import numpy as np
import ml_dtypes


def mxq(x, axis, fmt="e4m3"):
    dtype, down = {"e4m3": (ml_dtypes.float8_e4m3fn, 7), "e5m2": (ml_dtypes.float8_e5m2, 14)}[fmt]
    v = np.moveaxis(np.asarray(x, np.float32).astype(ml_dtypes.bfloat16).astype(np.float64), axis, -1)
    blocks = v.reshape(v.shape[:-1] + (-1, 32))
    amax = np.abs(blocks).max(-1, keepdims=True)
    byte = np.maximum(np.where(amax > 0, np.frexp(amax)[1] - 1 + 127, 0) - down, 1)
    scale = np.exp2(byte - 127.0)
    codes = (blocks / scale).astype(np.float32).astype(dtype).astype(np.float64)
    return np.moveaxis((codes * scale).reshape(v.shape), -1, axis)


WIDE = False


def mx_kscale(k):
    if not WIDE:
        return np.ones(k)
    levels = np.array([10, -10, 5, -5, 0])
    a = np.random.permutation(np.resize(levels, k // 512 * 4)).reshape(k // 512, 4)
    idx = np.arange(k)
    return np.exp2(a[idx // 512, idx % 128 // 32])


BF16 = ml_dtypes.bfloat16


def bf(x):
    return np.asarray(x, np.float32).astype(BF16)


def f64(x):
    return np.asarray(x).astype(np.float64)


B, CLS, N, D = 1, 2047, 2048, 512
KEEP = 0.75
CEN = 0.75


def pm(shape):
    return np.where(np.random.random(shape) < 0.5, 1.0, -1.0)


def setup_inputs():
    s = mx_kscale(D)
    feat = CEN * pm((B, N, 1)) * pm((B, 1, D)) + np.random.standard_normal((B, N, D))
    return {"feat": bf(feat * s),
            "mask": bf(np.random.random((B, N)) < KEEP),
            "W": bf(np.random.standard_normal((D, D)) / np.sqrt(D) / s[:, None]),
            "b": bf(np.random.standard_normal((N, D)) * 0.2)}


def reference(feat, mask, W, b):
    x, m = f64(feat), f64(mask)
    nrm = np.sqrt(np.sum(x * x, axis=1, keepdims=True))
    xn = x / np.maximum(nrm, 1e-12) * m[:, :, None]
    xq = mxq(xn, 2, "e4m3")
    edge = xq @ xq.transpose(0, 2, 1)
    A = (np.maximum(edge, 0.0) + np.eye(N)[None]) * m[:, None, :]
    d = np.power(A.sum(-1) + 1e-8, -0.5)
    adj = d[:, :, None] * A * d[:, None, :]
    pre_sup = mxq(x, 2, "e4m3") @ mxq(f64(W), 0, "e4m3")
    out = np.tanh((mxq(adj, 2, "e4m3") @ mxq(pre_sup, 1, "e4m3")) + f64(b)[None]) * m[:, :, None]
    return out.transpose(0, 2, 1)

@@ -1,0 +1,399 @@
+from contextlib import ExitStack
+
+import concourse.mybir as mybir
+from concourse.masks import make_identity
+
+F32 = mybir.dt.float32
+BF16 = mybir.dt.bfloat16
+U32 = mybir.dt.uint32
+U8 = mybir.dt.uint8
+FP8X4 = mybir.dt.float8_e4m3fn_x4
+ALU = mybir.AluOpType
+ACT = mybir.ActivationFunctionType
+AX = mybir.AxisListType
+
+P = 128
+N = 2048
+D = 512
+NT = N // P
+FLOPS = 2 * N * N * D * 2 + 2 * N * D * D
+ABLK = 8192
+
+
+def on_vector(c, nb):
+    return c + nb <= 2
+
+
+def round_blocks(g):
+    blocks = [(c, g) for c in range(g + 1)] + [(g, nb) for nb in range(g)]
+    return sorted(blocks, key=lambda cb: not on_vector(cb[0], cb[1]))
+
+
+def tile_graphlearner_pa_kernel(tc, feat, mask, W, b, out):
+    nc = tc.nc
+    feat_v = feat.flatten_outer_dims().rearrange("(t p) d -> p t d", p=P)
+    b_v = b.rearrange("(t p) e -> p t e", p=P)
+    mask_v = mask.rearrange("o (t p) -> (o t) p", p=P)
+    out_v = out.flatten_outer_dims().rearrange("(u r e) n -> u e r n", u=2, e=2)
+
+    with ExitStack() as ctx:
+        big = ctx.enter_context(tc.tile_pool(name="big", bufs=1))
+        keep = ctx.enter_context(tc.tile_pool(name="keep", bufs=1))
+        work = ctx.enter_context(tc.tile_pool(name="work", bufs=2))
+        psum = ctx.enter_context(tc.psum_pool(name="psum", bufs=8))
+        ctx.enter_context(tc.manual_schedule())
+
+        def bank(shape, name):
+            return psum.tile(shape, F32, name=name, tag="ps")
+
+        mraw = keep.tile([NT, P], BF16, name="mraw")
+        nc.sync.dma_start(out=mraw[:], in_=mask_v)
+        wraw = big.tile([P, 4, D], BF16, name="wraw", offset=13 * ABLK + 4096)
+        for u in range(2):
+            nc.sync.dma_start(
+                out=wraw[:, 2 * u:2 * u + 2, :],
+                in_=W[256 * u:256 * u + 256, :].rearrange("(q e) c -> q e c", e=2),
+            )
+        fraw = big.tile([P, NT, D], BF16, name="fraw", offset=14 * ABLK)
+        for k in range(4):
+            nc.sync.dma_start(out=fraw[:, 4 * k:4 * k + 4, :], in_=feat_v[:, 4 * k:4 * k + 4, :])
+
+        ident = keep.tile([P, P], F32, name="ident")
+        make_identity(nc, ident[:])
+        mhalf = keep.tile([P, 4], F32, name="mhalf")
+        nc.gpsimd.memset(mhalf[:], -0.5)
+        warm = keep.tile([P, 2], F32, name="warm")
+        nc.vector.memset(warm[:], 0.0)
+        nc.scalar.activation(out=warm[:, 1:2], in_=warm[:, 0:1], func=ACT.Tanh)
+
+        mpad = keep.tile([P, P], F32, name="mpad")
+        nc.vector.memset(mpad[:], 0.0)
+        nc.vector.tensor_copy(out=mpad[0:NT, :], in_=mraw[:])
+        mps = bank([P, P], "mps")
+        nc.tensor.transpose(mps[:], mpad[:], ident[:])
+        mcol = keep.tile([P, NT], F32, name="mcol")
+        nc.vector.tensor_copy(out=mcol[:], in_=mps[:, 0:NT])
+        diag = keep.tile([P, NT, P], F32, name="diag")
+        nc.gpsimd.tensor_tensor(
+            out=diag[:],
+            in0=ident[:].unsqueeze(1).to_broadcast([P, NT, P]),
+            in1=mcol[:].unsqueeze(2).to_broadcast([P, NT, P]),
+            op=ALU.mult,
+        )
+
+        xq = keep.tile([P, N], U32, name="xq", align_bytes=64)
+        xqs = keep.tile([P, N], U8, name="xqs", align_bytes=64)
+        pq = keep.tile([P, 4, D], U32, name="pq", align_bytes=64)
+        pqs = keep.tile([P, 4, D], U8, name="pqs", align_bytes=64)
+        fq = big.tile([P, N], U32, name="fq", offset=7 * ABLK, align_bytes=64)
+        fqs = big.tile([P, N], U8, name="fqs", offset=6 * ABLK, align_bytes=64)
+        wq = big.tile([P, D], U32, name="wq", offset=6 * ABLK + 2048, align_bytes=64)
+        wqs = big.tile([P, D], U8, name="wqs", offset=6 * ABLK + 4096, align_bytes=64)
+
+        wg = big.tile([P, D, 4], BF16, name="wg", offset=13 * ABLK, align_bytes=64)
+        wv = wraw[:].rearrange("p j (u r e) -> p u e r j", u=2, e=2)
+        for u in range(2):
+            for e in range(2):
+                eb = 2 * u + e
+                nc.vector.tensor_copy(out=wg[:, P * eb:P * eb + P, :], in_=wv[:, u, e])
+        nc.vector.quantize_mx(out=wq[:].bitcast(FP8X4), scales=wqs[:], in_=wg[:].rearrange("p w j -> p (w j)"))
+
+        gram = [bank([P, P], "gram%d" % k) for k in range(4)]
+        fgs = []
+
+        def quantise_feat(k):
+            nc.vector.quantize_mx(
+                out=fq[:, D * k:D * k + D].bitcast(FP8X4), scales=fqs[:, D * k:D * k + D], in_=fgs[k][:]
+            )
+
+        for k in range(4):
+            fg = big.tile([P, 4 * D], BF16, name="fg", tag="fg", bufs=4, offset=10 * ABLK, align_bytes=64)
+            fgs.append(fg)
+            fg32 = fg[:].bitcast(F32).rearrange("p (n u) -> p n u", u=2)
+            for t in range(4 * k, 4 * k + 4):
+                fv = fraw[:, t, :].rearrange("p (u q e) -> p u q e", u=2, e=2)
+                for u in range(2):
+                    for e in range(2):
+                        s = fv[:, u, :, e]
+                        nc.tensor.matmul(gram[2 * u + e][:], lhsT=s, rhs=s, start=(t == 0), stop=(t == NT - 1))
+            for hh in range(2):
+                tp = bank([P, 2, 256], "tp")
+                for tt in range(2):
+                    f32v = fraw[:, 4 * k + 2 * hh + tt, :].bitcast(F32)
+                    for u in range(2):
+                        nc.tensor.transpose(tp[:, u, P * tt:P * tt + P], f32v[:, P * u:P * u + P], ident[:])
+                nc.scalar.copy(out=fg32[:, 256 * hh:256 * hh + 256, :], in_=tp[:].rearrange("p u n -> p n u"))
+            if k < 2:
+                quantise_feat(k)
+
+        tms = {}
+
+        def masked_transposes(k):
+            for hh in range(2):
+                tm = bank([P, 2, 256], "tm")
+                tms[2 * k + hh] = tm
+                for tt in range(2):
+                    t = 4 * k + 2 * hh + tt
+                    f32v = fraw[:, t, :].bitcast(F32)
+                    for u in range(2):
+                        nc.tensor.transpose(tm[:, u, P * tt:P * tt + P], f32v[:, P * u:P * u + P], diag[:, t, :])
+
+        pgs = {}
+
+        def pre_sup(c):
+            pg = big.tile([P, D, 4], BF16, name="pg", tag="pg", bufs=4, offset=8 * ABLK, align_bytes=64)
+            pgs[c] = pg
+            for eb in range(4):
+                pp = bank([P, 4, P], "pp")
+                for j in range(4):
+                    i = 4 * c + j
+                    nc.tensor.matmul_mx(
+                        out=pp[:, j, :],
+                        lhsT=fq[:, P * i:P * i + P].bitcast(FP8X4),
+                        lhsT_scale=fqs[:, P * i:P * i + P],
+                        rhs=wq[:, P * eb:P * eb + P].bitcast(FP8X4),
+                        rhs_scale=wqs[:, P * eb:P * eb + P],
+                        start=True,
+                        stop=True,
+                    )
+                nc.scalar.copy(out=pg[:, P * eb:P * eb + P, :], in_=pp[:].rearrange("p j w -> p w j"))
+
+        def quantise_pre_sup(c):
+            nc.vector.quantize_mx(
+                out=pq[:, c, :].bitcast(FP8X4), scales=pqs[:, c, :], in_=pgs[c][:].rearrange("p w j -> p (w j)")
+            )
+
+        degs = keep.tile([P, NT, 4], F32, name="degs")
+        deg = keep.tile([P, NT], F32, name="deg")
+        dcol = keep.tile([P, NT], F32, name="dcol")
+        dbc = keep.tile([P, N], F32, name="dbc")
+        A = {}
+        aq = {}
+        aqs = {}
+
+        def edge_unit(c, nb):
+            A[(c, nb)] = big.tile([P, 4, D], F32, name="A%d_%d" % (c, nb), offset=(4 * c + nb) * ABLK)
+            for j in range(4):
+                i = 4 * c + j
+                ep = bank([P, D], "ep")
+                nc.tensor.matmul_mx(
+                    out=ep[:],
+                    lhsT=xq[:, P * i:P * i + P].bitcast(FP8X4),
+                    lhsT_scale=xqs[:, P * i:P * i + P],
+                    rhs=xq[:, D * nb:D * nb + D].bitcast(FP8X4),
+                    rhs_scale=xqs[:, D * nb:D * nb + D],
+                    start=True,
+                    stop=True,
+                )
+                nc.scalar.activation(
+                    out=A[(c, nb)][:, j, :], in_=ep[:], func=ACT.Relu, accum_out=degs[:, i, nb:nb + 1]
+                )
+            if nb == c:
+                for j in range(4):
+                    blk = A[(c, c)][:, j, P * j:P * j + P]
+                    nc.gpsimd.tensor_tensor(out=blk, in0=blk, in1=diag[:, 4 * c + j, :], op=ALU.add)
+
+        def edge_round(c):
+            for nb in [c] + [x for x in range(4) if x != c]:
+                edge_unit(c, nb)
+
+        masked_transposes(0)
+        masked_transposes(1)
+        junk = keep.tile([P, P], F32, name="junk")
+        n2 = keep.tile([P, 4], F32, name="n2")
+        for k in range(4):
+            nc.vector.scalar_tensor_tensor(
+                out=junk[:], in0=gram[k][:], scalar=1.0, in1=ident[:], op0=ALU.mult, op1=ALU.mult,
+                accum_out=n2[:, k:k + 1],
+            )
+        n2c = keep.tile([P, 4], F32, name="n2c")
+        nc.vector.tensor_scalar_max(out=n2c[:], in0=n2[:], scalar1=1e-24)
+        rn = keep.tile([P, 4], F32, name="rn")
+        nc.gpsimd.tensor_tensor(out=rn[:], in0=n2c[:], in1=mhalf[:], op=ALU.pow)
+        rn_b = rn[:].rearrange("p (u e) -> p u e", u=2).unsqueeze(1).to_broadcast([P, 256, 2, 2])
+        pre_sup(0)
+        pre_sup(1)
+
+        xgs = {}
+
+        def scale_xn(h):
+            k, hh = divmod(h, 2)
+            if hh == 0:
+                xgs[k] = big.tile([P, 4 * D], BF16, name="xg", tag="xg", bufs=2, offset=12 * ABLK, align_bytes=64)
+            xgv = xgs[k][:].rearrange("p (n u e) -> p n u e", u=2, e=2)
+            nc.vector.tensor_tensor(
+                out=xgv[:, 256 * hh:256 * hh + 256],
+                in0=tms[h][:].bitcast(BF16).rearrange("p u (n e) -> p n u e", e=2),
+                in1=rn_b,
+                op=ALU.mult,
+            )
+
+        def quantise_xn(k):
+            nc.vector.quantize_mx(
+                out=xq[:, D * k:D * k + D].bitcast(FP8X4), scales=xqs[:, D * k:D * k + D], in_=xgs[k][:]
+            )
+
+        scale_xn(0)
+        scale_xn(1)
+        masked_transposes(2)
+        scale_xn(2)
+        quantise_xn(0)
+        edge_unit(0, 0)
+        scale_xn(3)
+        masked_transposes(3)
+        scale_xn(4)
+        quantise_xn(1)
+        edge_unit(0, 1)
+        scale_xn(5)
+        scale_xn(6)
+        quantise_xn(2)
+        edge_unit(0, 2)
+        scale_xn(7)
+        quantise_xn(3)
+        edge_unit(0, 3)
+        quantise_feat(2)
+        quantise_feat(3)
+        pre_sup(2)
+        pre_sup(3)
+        quantise_pre_sup(0)
+        quantise_pre_sup(1)
+
+        def degrees(g):
+            cs = slice(4 * g, 4 * g + 4)
+            nc.vector.tensor_reduce(out=deg[:, cs], in_=degs[:, cs, :], axis=AX.X, op=ALU.add)
+            nc.vector.scalar_tensor_tensor(
+                out=deg[:, cs], in0=deg[:, cs], scalar=1e-8, in1=mcol[:, cs], op0=ALU.add, op1=ALU.add
+            )
+            nc.gpsimd.tensor_tensor(out=dcol[:, cs], in0=deg[:, cs], in1=mhalf[:], op=ALU.pow)
+
+        def scale_rows(c, nb):
+            for j in range(4):
+                row = A[(c, nb)][:, j, :]
+                dj = dcol[:, 4 * c + j:4 * c + j + 1]
+                if on_vector(c, nb):
+                    nc.vector.tensor_scalar_mul(out=row, in0=row, scalar1=dj)
+                else:
+                    nc.scalar.activation(out=row, in_=row, func=ACT.Copy, scale=dj)
+
+        def spread(g):
+            rep = work.tile([P, 4, P], F32, name="rep", tag="rep")
+            nc.vector.tensor_copy(out=rep[:], in_=dcol[:, 4 * g:4 * g + 4].unsqueeze(2).to_broadcast([P, 4, P]))
+            dp = bank([P, D], "dp")
+            for j in range(4):
+                nc.tensor.transpose(dp[:, P * j:P * j + P], rep[:, j, :], ident[:])
+            for nb in range(4):
+                if on_vector(g, nb):
+                    scale_rows(g, nb)
+            nc.vector.tensor_copy(out=dbc[:, D * g:D * g + D], in_=dp[:])
+
+        acc = {}
+
+        def passes(nb, c):
+            for et in range(4):
+                if c == 0:
+                    acc[(nb, et)] = bank([P, D], "acc")
+                nc.tensor.matmul_mx(
+                    out=acc[(nb, et)][:],
+                    lhsT=pq[:, c, P * et:P * et + P].bitcast(FP8X4),
+                    lhsT_scale=pqs[:, c, P * et:P * et + P],
+                    rhs=aq[(c, nb)][:].bitcast(FP8X4),
+                    rhs_scale=aqs[(c, nb)][:],
+                    start=(c == 0),
+                    stop=(c == 3),
+                )
+
+        scaled = []
+        quantised = []
+
+        def flush():
+            if len(quantised) < len(scaled):
+                c, nb, z = scaled[len(quantised)]
+                quantised.append((c, nb))
+                off = (4 * c + nb) * ABLK
+                aq[(c, nb)] = big.tile([P, D], U32, name="aq%d_%d" % (c, nb), offset=off, align_bytes=64)
+                aqs[(c, nb)] = big.tile([P, D], U8, name="aqs%d_%d" % (c, nb), offset=off + 2048, align_bytes=64)
+                nc.vector.quantize_mx(
+                    out=aq[(c, nb)][:].bitcast(FP8X4), scales=aqs[(c, nb)][:], in_=z[:].rearrange("p n j -> p (n j)")
+                )
+                if c == 3 or nb == 3:
+                    passes(nb, c)
+
+        def adj_block(c, nb):
+            z = work.tile([P, D, 4], BF16, name="z", tag="z", bufs=3, align_bytes=64)
+            nc.vector.tensor_tensor(
+                out=z[:],
+                in0=A[(c, nb)][:].rearrange("p j n -> p n j"),
+                in1=dbc[:, D * nb:D * nb + D].unsqueeze(2).to_broadcast([P, D, 4]),
+                op=ALU.mult,
+            )
+            flush()
+            scaled.append((c, nb, z))
+
+        edge_round(1)
+        degrees(0)
+        spread(0)
+        quantise_pre_sup(2)
+        quantise_pre_sup(3)
+        edge_round(2)
+        degrees(1)
+        adj_block(0, 0)
+        spread(1)
+        edge_round(3)
+        for g in (1, 2):
+            blocks = round_blocks(g)
+            for c, nb in blocks[:-1]:
+                adj_block(c, nb)
+            degrees(g + 1)
+            adj_block(blocks[-1][0], blocks[-1][1])
+            spread(g + 1)
+            if g == 1:
+                bT = keep.tile([P, 2, 2 * N], BF16, name="bT")
+                for c, nb in round_blocks(2):
+                    if not on_vector(c, nb):
+                        scale_rows(c, nb)
+                for k, cb in enumerate(round_blocks(0) + round_blocks(1)):
+                    braw = big.tile(
+                        [P, 4, D], BF16, name="braw%d" % k, offset=(4 * cb[0] + cb[1]) * ABLK + 4096
+                    )
+                    nc.sync.dma_start(out=braw[:], in_=b_v[:, 4 * k:4 * k + 4, :])
+                    for u in range(2):
+                        bp = bank([P, D], "bp")
+                        for tt in range(4):
+                            nc.tensor.transpose(
+                                bp[:, P * tt:P * tt + P],
+                                braw[:, tt, :].bitcast(F32)[:, P * u:P * u + P],
+                                diag[:, 4 * k + tt, :],
+                            )
+                        nc.scalar.copy(out=bT[:, u, 2 * D * k:2 * D * k + 2 * D], in_=bp[:].bitcast(BF16))
+                for c, nb in round_blocks(3):
+                    if c < 3:
+                        scale_rows(c, nb)
+        for c, nb in round_blocks(3):
+            if c == 3:
+                scale_rows(c, nb)
+
+        def finish(nb):
+            for u in range(2):
+                for e in range(2):
+                    y = work.tile([P, D], F32, name="y", tag="y", bufs=4)
+                    bview = bT[:, u, 2 * D * nb:2 * D * nb + 2 * D].rearrange("p (n e) -> p n e", e=2)
+                    nc.vector.tensor_tensor(out=y[:], in0=acc[(nb, 2 * u + e)][:], in1=bview[:, :, e], op=ALU.add)
+                    nc.scalar.activation(out=y[:], in_=y[:], func=ACT.Tanh)
+                    nc.sync.dma_start(out=out_v[u, e][:, D * nb:D * nb + D], in_=y[:])
+
+        def early_passes(nb):
+            for c in range(3):
+                passes(nb, c)
+
+        tail = round_blocks(3)
+        early_passes(0)
+        for c, nb in tail[:6]:
+            adj_block(c, nb)
+        finish(3)
+        early_passes(1)
+        adj_block(tail[6][0], tail[6][1])
+        finish(0)
+        early_passes(2)
+        flush()
+        finish(1)
+        finish(2)

@@ -18,15 +18,8 @@ D = 512
 NT = N // P
 FLOPS = 2 * N * N * D * 2 + 2 * N * D * D
 ABLK = 8192
-
-
-def on_vector(c, nb):
-    return c + nb <= 2
-
-
-def round_blocks(g):
-    blocks = [(c, g) for c in range(g + 1)] + [(g, nb) for nb in range(g)]
-    return sorted(blocks, key=lambda cb: not on_vector(cb[0], cb[1]))
+UPPER = [(c, nb) for c in range(4) for nb in range(c, 4)]
+EBASE = len(UPPER) * ABLK
 
 
 def tile_graphlearner_pa_kernel(tc, feat, mask, W, b, out):
@@ -43,23 +36,28 @@ def tile_graphlearner_pa_kernel(tc, feat, mask, W, b, out):
         psum = ctx.enter_context(tc.psum_pool(name="psum", bufs=8))
         ctx.enter_context(tc.manual_schedule())
 
-        def bank(shape, name):
-            return psum.tile(shape, F32, name=name, tag="ps")
+        def bank(shape, name, dtype=F32):
+            return psum.tile(shape, dtype, name=name, tag="ps")
+
+        def a_offset(c, nb):
+            return UPPER.index((c, nb)) * ABLK
 
         mraw = keep.tile([NT, P], BF16, name="mraw")
         nc.sync.dma_start(out=mraw[:], in_=mask_v)
-        wraw = big.tile([P, 4, D], BF16, name="wraw", offset=13 * ABLK + 4096)
+        wraw = big.tile([P, 4, D], BF16, name="wraw", offset=4 * ABLK + 4096)
         for u in range(2):
             nc.sync.dma_start(
                 out=wraw[:, 2 * u:2 * u + 2, :],
                 in_=W[256 * u:256 * u + 256, :].rearrange("(q e) c -> q e c", e=2),
             )
-        fraw = big.tile([P, NT, D], BF16, name="fraw", offset=14 * ABLK)
+        fraw = big.tile([P, NT, D], BF16, name="fraw", offset=7 * ABLK)
         for k in range(4):
             nc.sync.dma_start(out=fraw[:, 4 * k:4 * k + 4, :], in_=feat_v[:, 4 * k:4 * k + 4, :])
 
         ident = keep.tile([P, P], F32, name="ident")
         make_identity(nc, ident[:])
+        identb = keep.tile([P, P], BF16, name="identb")
+        make_identity(nc, identb[:])
         mhalf = keep.tile([P, 4], F32, name="mhalf")
         nc.gpsimd.memset(mhalf[:], -0.5)
         warm = keep.tile([P, 2], F32, name="warm")
@@ -74,7 +72,7 @@ def tile_graphlearner_pa_kernel(tc, feat, mask, W, b, out):
         mcol = keep.tile([P, NT], F32, name="mcol")
         nc.vector.tensor_copy(out=mcol[:], in_=mps[:, 0:NT])
         diag = keep.tile([P, NT, P], F32, name="diag")
-        nc.gpsimd.tensor_tensor(
+        nc.vector.tensor_tensor(
             out=diag[:],
             in0=ident[:].unsqueeze(1).to_broadcast([P, NT, P]),
             in1=mcol[:].unsqueeze(2).to_broadcast([P, NT, P]),
@@ -85,12 +83,12 @@ def tile_graphlearner_pa_kernel(tc, feat, mask, W, b, out):
         xqs = keep.tile([P, N], U8, name="xqs", align_bytes=64)
         pq = keep.tile([P, 4, D], U32, name="pq", align_bytes=64)
         pqs = keep.tile([P, 4, D], U8, name="pqs", align_bytes=64)
-        fq = big.tile([P, N], U32, name="fq", offset=7 * ABLK, align_bytes=64)
-        fqs = big.tile([P, N], U8, name="fqs", offset=6 * ABLK, align_bytes=64)
-        wq = big.tile([P, D], U32, name="wq", offset=6 * ABLK + 2048, align_bytes=64)
-        wqs = big.tile([P, D], U8, name="wqs", offset=6 * ABLK + 4096, align_bytes=64)
+        fq = big.tile([P, N], U32, name="fq", offset=EBASE, align_bytes=64)
+        fqs = big.tile([P, N], U8, name="fqs", offset=EBASE + 8192, align_bytes=64)
+        wq = big.tile([P, D], U32, name="wq", offset=EBASE + 10240, align_bytes=64)
+        wqs = big.tile([P, D], U8, name="wqs", offset=EBASE + 12288, align_bytes=64)
 
-        wg = big.tile([P, D, 4], BF16, name="wg", offset=13 * ABLK, align_bytes=64)
+        wg = big.tile([P, D, 4], BF16, name="wg", offset=4 * ABLK, align_bytes=64)
         wv = wraw[:].rearrange("p j (u r e) -> p u e r j", u=2, e=2)
         for u in range(2):
             for e in range(2):
@@ -107,7 +105,7 @@ def tile_graphlearner_pa_kernel(tc, feat, mask, W, b, out):
             )
 
         for k in range(4):
-            fg = big.tile([P, 4 * D], BF16, name="fg", tag="fg", bufs=4, offset=10 * ABLK, align_bytes=64)
+            fg = big.tile([P, 4 * D], BF16, name="fg", tag="fg", bufs=4, offset=5 * ABLK, align_bytes=64)
             fgs.append(fg)
             fg32 = fg[:].bitcast(F32).rearrange("p (n u) -> p n u", u=2)
             for t in range(4 * k, 4 * k + 4):
@@ -141,7 +139,7 @@ def tile_graphlearner_pa_kernel(tc, feat, mask, W, b, out):
         pgs = {}
 
         def pre_sup(c):
-            pg = big.tile([P, D, 4], BF16, name="pg", tag="pg", bufs=4, offset=8 * ABLK, align_bytes=64)
+            pg = big.tile([P, D, 4], BF16, name="pg", tag="pg", bufs=4, offset=EBASE + 13312, align_bytes=64)
             pgs[c] = pg
             for eb in range(4):
                 pp = bank([P, 4, P], "pp")
@@ -172,7 +170,8 @@ def tile_graphlearner_pa_kernel(tc, feat, mask, W, b, out):
         aqs = {}
 
         def edge_unit(c, nb):
-            A[(c, nb)] = big.tile([P, 4, D], F32, name="A%d_%d" % (c, nb), offset=(4 * c + nb) * ABLK)
+            if nb >= c:
+                A[(c, nb)] = big.tile([P, 4, D], F32, name="A%d_%d" % (c, nb), offset=a_offset(c, nb))
             for j in range(4):
                 i = 4 * c + j
                 ep = bank([P, D], "ep")
@@ -185,16 +184,20 @@ def tile_graphlearner_pa_kernel(tc, feat, mask, W, b, out):
                     start=True,
                     stop=True,
                 )
-                nc.scalar.activation(
-                    out=A[(c, nb)][:, j, :], in_=ep[:], func=ACT.Relu, accum_out=degs[:, i, nb:nb + 1]
-                )
-            if nb == c:
-                for j in range(4):
-                    blk = A[(c, c)][:, j, P * j:P * j + P]
-                    nc.gpsimd.tensor_tensor(out=blk, in0=blk, in1=diag[:, 4 * c + j, :], op=ALU.add)
+                if nb >= c:
+                    row = A[(c, nb)][:, j, :]
+                else:
+                    unused = work.tile([P, D], BF16, name="unused", tag="unused")
+                    row = unused[:]
+                nc.scalar.activation(out=row, in_=ep[:], func=ACT.Relu, accum_out=degs[:, i, nb:nb + 1])
 
-        def edge_round(c):
-            for nb in [c] + [x for x in range(4) if x != c]:
+        def self_loops(c):
+            for j in range(4):
+                blk = A[(c, c)][:, j, P * j:P * j + P]
+                nc.vector.tensor_tensor(out=blk, in0=blk, in1=diag[:, 4 * c + j, :], op=ALU.add)
+
+        def edge_round(c, part=slice(0, 4)):
+            for nb in ([c] + [x for x in range(4) if x != c])[part]:
                 edge_unit(c, nb)
 
         masked_transposes(0)
@@ -219,7 +222,7 @@ def tile_graphlearner_pa_kernel(tc, feat, mask, W, b, out):
         def scale_xn(h):
             k, hh = divmod(h, 2)
             if hh == 0:
-                xgs[k] = big.tile([P, 4 * D], BF16, name="xg", tag="xg", bufs=2, offset=12 * ABLK, align_bytes=64)
+                xgs[k] = big.tile([P, 4 * D], BF16, name="xg", tag="xg", bufs=2, offset=9 * ABLK, align_bytes=64)
             xgv = xgs[k][:].rearrange("p (n u e) -> p n u e", u=2, e=2)
             nc.vector.tensor_tensor(
                 out=xgv[:, 256 * hh:256 * hh + 256],
@@ -253,8 +256,6 @@ def tile_graphlearner_pa_kernel(tc, feat, mask, W, b, out):
         edge_unit(0, 3)
         quantise_feat(2)
         quantise_feat(3)
-        pre_sup(2)
-        pre_sup(3)
         quantise_pre_sup(0)
         quantise_pre_sup(1)
 
@@ -266,134 +267,150 @@ def tile_graphlearner_pa_kernel(tc, feat, mask, W, b, out):
             )
             nc.gpsimd.tensor_tensor(out=dcol[:, cs], in0=deg[:, cs], in1=mhalf[:], op=ALU.pow)
 
-        def scale_rows(c, nb):
-            for j in range(4):
-                row = A[(c, nb)][:, j, :]
-                dj = dcol[:, 4 * c + j:4 * c + j + 1]
-                if on_vector(c, nb):
-                    nc.vector.tensor_scalar_mul(out=row, in0=row, scalar1=dj)
-                else:
-                    nc.scalar.activation(out=row, in_=row, func=ACT.Copy, scale=dj)
-
-        def spread(g):
+        def spread(g, meanwhile=()):
             rep = work.tile([P, 4, P], F32, name="rep", tag="rep")
             nc.vector.tensor_copy(out=rep[:], in_=dcol[:, 4 * g:4 * g + 4].unsqueeze(2).to_broadcast([P, 4, P]))
             dp = bank([P, D], "dp")
             for j in range(4):
                 nc.tensor.transpose(dp[:, P * j:P * j + P], rep[:, j, :], ident[:])
-            for nb in range(4):
-                if on_vector(g, nb):
-                    scale_rows(g, nb)
+            self_loops(g)
+            for nb in range(g, 4):
+                for j in range(4):
+                    row = A[(g, nb)][:, j, :]
+                    nc.vector.tensor_scalar_mul(out=row, in0=row, scalar1=dcol[:, 4 * g + j:4 * g + j + 1])
+            for job in meanwhile:
+                job()
             nc.vector.tensor_copy(out=dbc[:, D * g:D * g + D], in_=dp[:])
 
-        acc = {}
+        zs = {}
 
-        def passes(nb, c):
-            for et in range(4):
-                if c == 0:
-                    acc[(nb, et)] = bank([P, D], "acc")
-                nc.tensor.matmul_mx(
-                    out=acc[(nb, et)][:],
-                    lhsT=pq[:, c, P * et:P * et + P].bitcast(FP8X4),
-                    lhsT_scale=pqs[:, c, P * et:P * et + P],
-                    rhs=aq[(c, nb)][:].bitcast(FP8X4),
-                    rhs_scale=aqs[(c, nb)][:],
-                    start=(c == 0),
-                    stop=(c == 3),
-                )
-
-        scaled = []
-        quantised = []
-
-        def flush():
-            if len(quantised) < len(scaled):
-                c, nb, z = scaled[len(quantised)]
-                quantised.append((c, nb))
-                off = (4 * c + nb) * ABLK
+        def quantise(c, nb):
+            if nb >= c:
+                off = a_offset(c, nb)
                 aq[(c, nb)] = big.tile([P, D], U32, name="aq%d_%d" % (c, nb), offset=off, align_bytes=64)
                 aqs[(c, nb)] = big.tile([P, D], U8, name="aqs%d_%d" % (c, nb), offset=off + 2048, align_bytes=64)
-                nc.vector.quantize_mx(
-                    out=aq[(c, nb)][:].bitcast(FP8X4), scales=aqs[(c, nb)][:], in_=z[:].rearrange("p n j -> p (n j)")
-                )
-                if c == 3 or nb == 3:
-                    passes(nb, c)
+            else:
+                aq[(c, nb)] = keep.tile([P, D], U32, name="aq%d_%d" % (c, nb), align_bytes=64)
+                aqs[(c, nb)] = keep.tile([P, D], U8, name="aqs%d_%d" % (c, nb), align_bytes=64)
+            nc.vector.quantize_mx(
+                out=aq[(c, nb)][:].bitcast(FP8X4),
+                scales=aqs[(c, nb)][:],
+                in_=zs[(c, nb)][:].rearrange("p n j -> p (n j)"),
+            )
 
-        def adj_block(c, nb):
-            z = work.tile([P, D, 4], BF16, name="z", tag="z", bufs=3, align_bytes=64)
+        def scale_columns(c, nb):
+            z = work.tile([P, D, 4], BF16, name="z", tag="z", bufs=4, align_bytes=64)
+            zs[(c, nb)] = z
             nc.vector.tensor_tensor(
                 out=z[:],
                 in0=A[(c, nb)][:].rearrange("p j n -> p n j"),
                 in1=dbc[:, D * nb:D * nb + D].unsqueeze(2).to_broadcast([P, D, 4]),
                 op=ALU.mult,
             )
-            flush()
-            scaled.append((c, nb, z))
+
+        def mirror(c, nb):
+            z = zs[(c, nb)]
+            zm = work.tile([P, D, 4], BF16, name="zm", tag="zm", bufs=3, align_bytes=64)
+            zs[(nb, c)] = zm
+            for h in range(2):
+                tb = bank([P, 4, 256], "tb", BF16)
+                for j in range(4):
+                    for jj in (2 * h, 2 * h + 1):
+                        nc.tensor.transpose(
+                            tb[:, j, P * (jj - 2 * h):P * (jj - 2 * h) + P], z[:, P * j:P * j + P, jj], identb[:]
+                        )
+                nc.scalar.copy(out=zm[:, 256 * h:256 * h + 256, :], in_=tb[:].rearrange("p j n -> p n j"))
+
+        def adj_round(g):
+            for c in range(g + 1):
+                scale_columns(c, g)
+                if c < g:
+                    mirror(c, g)
+                if c > 0:
+                    quantise(c - 1, g)
+            quantise(g, g)
+
+        def mirrors_of(g):
+            for c in range(g):
+                quantise(g, c)
 
         edge_round(1)
         degrees(0)
         spread(0)
-        quantise_pre_sup(2)
-        quantise_pre_sup(3)
-        edge_round(2)
+        edge_round(2, slice(0, 2))
+        adj_round(0)
         degrees(1)
-        adj_block(0, 0)
         spread(1)
-        edge_round(3)
-        for g in (1, 2):
-            blocks = round_blocks(g)
-            for c, nb in blocks[:-1]:
-                adj_block(c, nb)
-            degrees(g + 1)
-            adj_block(blocks[-1][0], blocks[-1][1])
-            spread(g + 1)
-            if g == 1:
-                bT = keep.tile([P, 2, 2 * N], BF16, name="bT")
-                for c, nb in round_blocks(2):
-                    if not on_vector(c, nb):
-                        scale_rows(c, nb)
-                for k, cb in enumerate(round_blocks(0) + round_blocks(1)):
-                    braw = big.tile(
-                        [P, 4, D], BF16, name="braw%d" % k, offset=(4 * cb[0] + cb[1]) * ABLK + 4096
+        edge_round(2, slice(2, 4))
+        edge_round(3, slice(0, 2))
+        adj_round(1)
+        degrees(2)
+        spread(2)
+        edge_round(3, slice(2, 4))
+        adj_round(2)
+        pre_sup(2)
+        pre_sup(3)
+        degrees(3)
+        spread(3, [lambda: mirrors_of(1), lambda: mirrors_of(2), lambda: quantise_pre_sup(2), lambda: quantise_pre_sup(3)])
+
+        bT = keep.tile([P, 2, 2 * N], BF16, name="bT")
+        for k in range(4):
+            braw = big.tile([P, 4, D], BF16, name="braw%d" % k, offset=EBASE + 4096 * k)
+            nc.sync.dma_start(out=braw[:], in_=b_v[:, 4 * k:4 * k + 4, :])
+            for u in range(2):
+                bp = bank([P, D], "bp")
+                for tt in range(4):
+                    nc.tensor.transpose(
+                        bp[:, P * tt:P * tt + P], braw[:, tt, :].bitcast(F32)[:, P * u:P * u + P], diag[:, 4 * k + tt, :]
                     )
-                    nc.sync.dma_start(out=braw[:], in_=b_v[:, 4 * k:4 * k + 4, :])
-                    for u in range(2):
-                        bp = bank([P, D], "bp")
-                        for tt in range(4):
-                            nc.tensor.transpose(
-                                bp[:, P * tt:P * tt + P],
-                                braw[:, tt, :].bitcast(F32)[:, P * u:P * u + P],
-                                diag[:, 4 * k + tt, :],
-                            )
-                        nc.scalar.copy(out=bT[:, u, 2 * D * k:2 * D * k + 2 * D], in_=bp[:].bitcast(BF16))
-                for c, nb in round_blocks(3):
-                    if c < 3:
-                        scale_rows(c, nb)
-        for c, nb in round_blocks(3):
-            if c == 3:
-                scale_rows(c, nb)
+                nc.scalar.copy(out=bT[:, u, 2 * D * k:2 * D * k + 2 * D], in_=bp[:].bitcast(BF16))
+
+        acc = {}
+
+        def passes(nb, cs):
+            for c in cs:
+                for et in range(4):
+                    if c == 0:
+                        acc[(nb, et)] = bank([P, D], "acc")
+                    nc.tensor.matmul_mx(
+                        out=acc[(nb, et)][:],
+                        lhsT=pq[:, c, P * et:P * et + P].bitcast(FP8X4),
+                        lhsT_scale=pqs[:, c, P * et:P * et + P],
+                        rhs=aq[(c, nb)][:].bitcast(FP8X4),
+                        rhs_scale=aqs[(c, nb)][:],
+                        start=(c == 0),
+                        stop=(c == 3),
+                    )
 
         def finish(nb):
             for u in range(2):
                 for e in range(2):
-                    y = work.tile([P, D], F32, name="y", tag="y", bufs=4)
+                    y = work.tile([P, D], F32, name="y", tag="y", bufs=6)
                     bview = bT[:, u, 2 * D * nb:2 * D * nb + 2 * D].rearrange("p (n e) -> p n e", e=2)
                     nc.vector.tensor_tensor(out=y[:], in0=acc[(nb, 2 * u + e)][:], in1=bview[:, :, e], op=ALU.add)
                     nc.scalar.activation(out=y[:], in_=y[:], func=ACT.Tanh)
                     nc.sync.dma_start(out=out_v[u, e][:, D * nb:D * nb + D], in_=y[:])
 
-        def early_passes(nb):
-            for c in range(3):
-                passes(nb, c)
-
-        tail = round_blocks(3)
-        early_passes(0)
-        for c, nb in tail[:6]:
-            adj_block(c, nb)
-        finish(3)
-        early_passes(1)
-        adj_block(tail[6][0], tail[6][1])
+        passes(0, range(3))
+        scale_columns(0, 3)
+        mirror(0, 3)
+        scale_columns(1, 3)
+        mirror(1, 3)
+        quantise(0, 3)
+        scale_columns(2, 3)
+        mirror(2, 3)
+        quantise(1, 3)
+        quantise(3, 0)
+        passes(0, [3])
+        scale_columns(3, 3)
+        quantise(2, 3)
+        quantise(3, 1)
+        passes(1, range(4))
+        quantise(3, 3)
         finish(0)
-        early_passes(2)
-        flush()
+        passes(3, range(4))
+        quantise(3, 2)
         finish(1)
+        passes(2, range(4))
+        finish(3)
         finish(2)

@@ -302,9 +302,9 @@ def tile_graphlearner_pa_kernel(tc, feat, mask, W, b, out):
             z = work.tile([P, D, 4], BF16, name="z", tag="z", bufs=4, align_bytes=64)
             zs[(c, nb)] = z
             nc.vector.tensor_tensor(
-                out=z[:],
-                in0=A[(c, nb)][:].rearrange("p j n -> p n j"),
-                in1=dbc[:, D * nb:D * nb + D].unsqueeze(2).to_broadcast([P, D, 4]),
+                out=z[:].rearrange("p (c i) j -> p c j i", i=4),
+                in0=A[(c, nb)][:].rearrange("p j (c i) -> p c j i", i=4),
+                in1=dbc[:, D * nb:D * nb + D].rearrange("p (c i) -> p c i", i=4).unsqueeze(2).to_broadcast([P, P, 4, 4]),
                 op=ALU.mult,
             )
 

@@ -58,11 +58,9 @@ def tile_graphlearner_pa_kernel(tc, feat, mask, W, b, out):
         make_identity(nc, ident[:])
         identb = keep.tile([P, P], BF16, name="identb")
         make_identity(nc, identb[:])
-        mhalf = keep.tile([P, 4], F32, name="mhalf")
-        nc.gpsimd.memset(mhalf[:], -0.5)
         warm = keep.tile([P, 2], F32, name="warm")
-        nc.vector.memset(warm[:], 0.0)
-        nc.scalar.activation(out=warm[:, 1:2], in_=warm[:, 0:1], func=ACT.Tanh)
+        nc.vector.memset(warm[:], 1.0)
+        nc.scalar.sqrt(out=warm[:, 1:2], in_=warm[:, 0:1])
 
         mpad = keep.tile([P, P], F32, name="mpad")
         nc.vector.memset(mpad[:], 0.0)
@@ -138,7 +136,7 @@ def tile_graphlearner_pa_kernel(tc, feat, mask, W, b, out):
 
         pgs = {}
 
-        def pre_sup(c):
+        def pre_sup(c, engine):
             pg = big.tile([P, D, 4], BF16, name="pg", tag="pg", bufs=4, offset=EBASE + 13312, align_bytes=64)
             pgs[c] = pg
             for eb in range(4):
@@ -154,15 +152,18 @@ def tile_graphlearner_pa_kernel(tc, feat, mask, W, b, out):
                         start=True,
                         stop=True,
                     )
-                nc.scalar.copy(out=pg[:, P * eb:P * eb + P, :], in_=pp[:].rearrange("p j w -> p w j"))
+                engine(out=pg[:, P * eb:P * eb + P, :], in_=pp[:].rearrange("p j w -> p w j"))
 
         def quantise_pre_sup(c):
             nc.vector.quantize_mx(
                 out=pq[:, c, :].bitcast(FP8X4), scales=pqs[:, c, :], in_=pgs[c][:].rearrange("p w j -> p (w j)")
             )
 
-        degs = keep.tile([P, NT, 4], F32, name="degs")
+        degs = keep.tile([P, NT, 5], F32, name="degs")
+        nc.scalar.add(out=degs[:, :, 4], in_=mcol[:], add=1e-8)
         deg = keep.tile([P, NT], F32, name="deg")
+        sdeg = keep.tile([P, NT], F32, name="sdeg")
+        five = keep.tile([P, 5], F32, name="five")
         dcol = keep.tile([P, NT], F32, name="dcol")
         dbc = keep.tile([P, N], F32, name="dbc")
         A = {}
@@ -211,11 +212,13 @@ def tile_graphlearner_pa_kernel(tc, feat, mask, W, b, out):
             )
         n2c = keep.tile([P, 4], F32, name="n2c")
         nc.vector.tensor_scalar_max(out=n2c[:], in0=n2[:], scalar1=1e-24)
+        nrm = keep.tile([P, 4], F32, name="nrm")
+        nc.scalar.sqrt(out=nrm[:], in_=n2c[:])
         rn = keep.tile([P, 4], F32, name="rn")
-        nc.gpsimd.tensor_tensor(out=rn[:], in0=n2c[:], in1=mhalf[:], op=ALU.pow)
+        nc.vector.reciprocal(out=rn[:], in_=nrm[:])
         rn_b = rn[:].rearrange("p (u e) -> p u e", u=2).unsqueeze(1).to_broadcast([P, 256, 2, 2])
-        pre_sup(0)
-        pre_sup(1)
+        pre_sup(0, nc.scalar.copy)
+        pre_sup(1, nc.scalar.copy)
 
         xgs = {}
 
@@ -257,17 +260,18 @@ def tile_graphlearner_pa_kernel(tc, feat, mask, W, b, out):
         quantise_feat(2)
         quantise_feat(3)
         quantise_pre_sup(0)
+        pre_sup(2, nc.vector.tensor_copy)
         quantise_pre_sup(1)
+        pre_sup(3, nc.vector.tensor_copy)
+        quantise_pre_sup(2)
 
         def degrees(g):
-            cs = slice(4 * g, 4 * g + 4)
-            nc.vector.tensor_reduce(out=deg[:, cs], in_=degs[:, cs, :], axis=AX.X, op=ALU.add)
-            nc.vector.scalar_tensor_tensor(
-                out=deg[:, cs], in0=deg[:, cs], scalar=1e-8, in1=mcol[:, cs], op0=ALU.add, op1=ALU.add
-            )
-            nc.gpsimd.tensor_tensor(out=dcol[:, cs], in0=deg[:, cs], in1=mhalf[:], op=ALU.pow)
+            for i in range(4 * g, 4 * g + 4):
+                nc.scalar.activation(out=five[:], in_=degs[:, i, :], func=ACT.Copy, accum_out=deg[:, i:i + 1])
+            nc.scalar.sqrt(out=sdeg[:, 4 * g:4 * g + 4], in_=deg[:, 4 * g:4 * g + 4])
 
         def spread(g, meanwhile=()):
+            nc.vector.reciprocal(out=dcol[:, 4 * g:4 * g + 4], in_=sdeg[:, 4 * g:4 * g + 4])
             rep = work.tile([P, 4, P], F32, name="rep", tag="rep")
             nc.vector.tensor_copy(out=rep[:], in_=dcol[:, 4 * g:4 * g + 4].unsqueeze(2).to_broadcast([P, 4, P]))
             dp = bank([P, D], "dp")
@@ -334,24 +338,23 @@ def tile_graphlearner_pa_kernel(tc, feat, mask, W, b, out):
             for c in range(g):
                 quantise(g, c)
 
-        edge_round(1)
         degrees(0)
+        edge_round(1)
+        degrees(1)
+        quantise_pre_sup(3)
         spread(0)
         edge_round(2, slice(0, 2))
         adj_round(0)
-        degrees(1)
         spread(1)
         edge_round(2, slice(2, 4))
+        degrees(2)
         edge_round(3, slice(0, 2))
         adj_round(1)
-        degrees(2)
         spread(2)
         edge_round(3, slice(2, 4))
-        adj_round(2)
-        pre_sup(2)
-        pre_sup(3)
         degrees(3)
-        spread(3, [lambda: mirrors_of(1), lambda: mirrors_of(2), lambda: quantise_pre_sup(2), lambda: quantise_pre_sup(3)])
+        adj_round(2)
+        spread(3, [lambda: mirrors_of(1), lambda: mirrors_of(2)])
 
         bT = keep.tile([P, 2, 2 * N], BF16, name="bT")
         for k in range(4):
@@ -385,7 +388,7 @@ def tile_graphlearner_pa_kernel(tc, feat, mask, W, b, out):
         def finish(nb):
             for u in range(2):
                 for e in range(2):
-                    y = work.tile([P, D], F32, name="y", tag="y", bufs=6)
+                    y = work.tile([P, D], F32, name="y", tag="y", bufs=8)
                     bview = bT[:, u, 2 * D * nb:2 * D * nb + 2 * D].rearrange("p (n e) -> p n e", e=2)
                     nc.vector.tensor_tensor(out=y[:], in0=acc[(nb, 2 * u + e)][:], in1=bview[:, :, e], op=ALU.add)
                     nc.scalar.activation(out=y[:], in_=y[:], func=ACT.Tanh)

@@ -56,8 +56,6 @@ def tile_graphlearner_pa_kernel(tc, feat, mask, W, b, out):
 
         ident = keep.tile([P, P], F32, name="ident")
         make_identity(nc, ident[:])
-        identb = keep.tile([P, P], BF16, name="identb")
-        make_identity(nc, identb[:])
         warm = keep.tile([P, 2], F32, name="warm")
         nc.vector.memset(warm[:], 1.0)
         nc.scalar.sqrt(out=warm[:, 1:2], in_=warm[:, 0:1])
@@ -278,10 +276,9 @@ def tile_graphlearner_pa_kernel(tc, feat, mask, W, b, out):
             for j in range(4):
                 nc.tensor.transpose(dp[:, P * j:P * j + P], rep[:, j, :], ident[:])
             self_loops(g)
-            for nb in range(g, 4):
-                for j in range(4):
-                    row = A[(g, nb)][:, j, :]
-                    nc.vector.tensor_scalar_mul(out=row, in0=row, scalar1=dcol[:, 4 * g + j:4 * g + j + 1])
+            for j in range(4):
+                row = A[(g, 3)][:, j, :]
+                nc.vector.tensor_scalar_mul(out=row, in0=row, scalar1=dcol[:, 4 * g + j:4 * g + j + 1])
             for job in meanwhile:
                 job()
             nc.vector.tensor_copy(out=dbc[:, D * g:D * g + D], in_=dp[:])
@@ -289,13 +286,9 @@ def tile_graphlearner_pa_kernel(tc, feat, mask, W, b, out):
         zs = {}
 
         def quantise(c, nb):
-            if nb >= c:
-                off = a_offset(c, nb)
-                aq[(c, nb)] = big.tile([P, D], U32, name="aq%d_%d" % (c, nb), offset=off, align_bytes=64)
-                aqs[(c, nb)] = big.tile([P, D], U8, name="aqs%d_%d" % (c, nb), offset=off + 2048, align_bytes=64)
-            else:
-                aq[(c, nb)] = keep.tile([P, D], U32, name="aq%d_%d" % (c, nb), align_bytes=64)
-                aqs[(c, nb)] = keep.tile([P, D], U8, name="aqs%d_%d" % (c, nb), align_bytes=64)
+            off = a_offset(c, nb) if nb >= c else a_offset(nb, c) + 4096
+            aq[(c, nb)] = big.tile([P, D], U32, name="aq%d_%d" % (c, nb), offset=off, align_bytes=64)
+            aqs[(c, nb)] = big.tile([P, D], U8, name="aqs%d_%d" % (c, nb), offset=off + 2048, align_bytes=64)
             nc.vector.quantize_mx(
                 out=aq[(c, nb)][:].bitcast(FP8X4),
                 scales=aqs[(c, nb)][:],
@@ -305,6 +298,21 @@ def tile_graphlearner_pa_kernel(tc, feat, mask, W, b, out):
         def scale_columns(c, nb):
             z = work.tile([P, D, 4], BF16, name="z", tag="z", bufs=4, align_bytes=64)
             zs[(c, nb)] = z
+            if nb < 3:
+                y = work.tile([P, 4, D], BF16, name="yy", tag="yy", bufs=2)
+                for j in range(4):
+                    nc.vector.scalar_tensor_tensor(
+                        out=y[:, j, :],
+                        in0=A[(c, nb)][:, j, :],
+                        scalar=dcol[:, 4 * c + j:4 * c + j + 1],
+                        in1=dbc[:, D * nb:D * nb + D],
+                        op0=ALU.mult,
+                        op1=ALU.mult,
+                    )
+                nc.vector.tensor_copy(
+                    out=z[:].rearrange("p (c i) j -> p c j i", i=4), in_=y[:].rearrange("p j (c i) -> p c j i", i=4)
+                )
+                return
             nc.vector.tensor_tensor(
                 out=z[:].rearrange("p (c i) j -> p c j i", i=4),
                 in0=A[(c, nb)][:].rearrange("p j (c i) -> p c j i", i=4),
@@ -316,14 +324,15 @@ def tile_graphlearner_pa_kernel(tc, feat, mask, W, b, out):
             z = zs[(c, nb)]
             zm = work.tile([P, D, 4], BF16, name="zm", tag="zm", bufs=3, align_bytes=64)
             zs[(nb, c)] = zm
-            for h in range(2):
-                tb = bank([P, 4, 256], "tb", BF16)
+            z32 = z[:].rearrange("p n j -> p (n j)").bitcast(F32).rearrange("p (n w) -> p n w", w=2)
+            for w in range(2):
+                tb = bank([P, 4, P], "tb")
                 for j in range(4):
-                    for jj in (2 * h, 2 * h + 1):
-                        nc.tensor.transpose(
-                            tb[:, j, P * (jj - 2 * h):P * (jj - 2 * h) + P], z[:, P * j:P * j + P, jj], identb[:]
-                        )
-                nc.scalar.copy(out=zm[:, 256 * h:256 * h + 256, :], in_=tb[:].rearrange("p j n -> p n j"))
+                    nc.tensor.transpose(tb[:, j, :], z32[:, P * j:P * j + P, w], ident[:])
+                nc.scalar.copy(
+                    out=zm[:, 256 * w:256 * w + 256, :].rearrange("p (e q) j -> p e q j", e=2),
+                    in_=tb[:].bitcast(BF16).rearrange("p j (q e) -> p e q j", e=2),
+                )
 
         def adj_round(g):
             for c in range(g + 1):

@@ -34,7 +34,6 @@ def tile_graphlearner_pa_kernel(tc, feat, mask, W, b, out):
         keep = ctx.enter_context(tc.tile_pool(name="keep", bufs=1))
         work = ctx.enter_context(tc.tile_pool(name="work", bufs=2))
         psum = ctx.enter_context(tc.psum_pool(name="psum", bufs=8))
-        ctx.enter_context(tc.manual_schedule())
 
         def bank(shape, name, dtype=F32):
             return psum.tile(shape, dtype, name=name, tag="ps")
@@ -56,6 +55,8 @@ def tile_graphlearner_pa_kernel(tc, feat, mask, W, b, out):
 
         ident = keep.tile([P, P], F32, name="ident")
         make_identity(nc, ident[:])
+        identb = keep.tile([P, P], BF16, name="identb")
+        make_identity(nc, identb[:])
         warm = keep.tile([P, 2], F32, name="warm")
         nc.vector.memset(warm[:], 1.0)
         nc.scalar.sqrt(out=warm[:, 1:2], in_=warm[:, 0:1])
@@ -276,9 +277,10 @@ def tile_graphlearner_pa_kernel(tc, feat, mask, W, b, out):
             for j in range(4):
                 nc.tensor.transpose(dp[:, P * j:P * j + P], rep[:, j, :], ident[:])
             self_loops(g)
-            for j in range(4):
-                row = A[(g, 3)][:, j, :]
-                nc.vector.tensor_scalar_mul(out=row, in0=row, scalar1=dcol[:, 4 * g + j:4 * g + j + 1])
+            for nb in range(g, 4):
+                for j in range(4):
+                    row = A[(g, nb)][:, j, :]
+                    nc.vector.tensor_scalar_mul(out=row, in0=row, scalar1=dcol[:, 4 * g + j:4 * g + j + 1])
             for job in meanwhile:
                 job()
             nc.vector.tensor_copy(out=dbc[:, D * g:D * g + D], in_=dp[:])
@@ -286,9 +288,13 @@ def tile_graphlearner_pa_kernel(tc, feat, mask, W, b, out):
         zs = {}
 
         def quantise(c, nb):
-            off = a_offset(c, nb) if nb >= c else a_offset(nb, c) + 4096
-            aq[(c, nb)] = big.tile([P, D], U32, name="aq%d_%d" % (c, nb), offset=off, align_bytes=64)
-            aqs[(c, nb)] = big.tile([P, D], U8, name="aqs%d_%d" % (c, nb), offset=off + 2048, align_bytes=64)
+            if nb >= c:
+                off = a_offset(c, nb)
+                aq[(c, nb)] = big.tile([P, D], U32, name="aq%d_%d" % (c, nb), offset=off, align_bytes=64)
+                aqs[(c, nb)] = big.tile([P, D], U8, name="aqs%d_%d" % (c, nb), offset=off + 2048, align_bytes=64)
+            else:
+                aq[(c, nb)] = keep.tile([P, D], U32, name="aq%d_%d" % (c, nb), align_bytes=64)
+                aqs[(c, nb)] = keep.tile([P, D], U8, name="aqs%d_%d" % (c, nb), align_bytes=64)
             nc.vector.quantize_mx(
                 out=aq[(c, nb)][:].bitcast(FP8X4),
                 scales=aqs[(c, nb)][:],
@@ -298,21 +304,6 @@ def tile_graphlearner_pa_kernel(tc, feat, mask, W, b, out):
         def scale_columns(c, nb):
             z = work.tile([P, D, 4], BF16, name="z", tag="z", bufs=4, align_bytes=64)
             zs[(c, nb)] = z
-            if nb < 3:
-                y = work.tile([P, 4, D], BF16, name="yy", tag="yy", bufs=2)
-                for j in range(4):
-                    nc.vector.scalar_tensor_tensor(
-                        out=y[:, j, :],
-                        in0=A[(c, nb)][:, j, :],
-                        scalar=dcol[:, 4 * c + j:4 * c + j + 1],
-                        in1=dbc[:, D * nb:D * nb + D],
-                        op0=ALU.mult,
-                        op1=ALU.mult,
-                    )
-                nc.vector.tensor_copy(
-                    out=z[:].rearrange("p (c i) j -> p c j i", i=4), in_=y[:].rearrange("p j (c i) -> p c j i", i=4)
-                )
-                return
             nc.vector.tensor_tensor(
                 out=z[:].rearrange("p (c i) j -> p c j i", i=4),
                 in0=A[(c, nb)][:].rearrange("p j (c i) -> p c j i", i=4),
@@ -324,15 +315,14 @@ def tile_graphlearner_pa_kernel(tc, feat, mask, W, b, out):
             z = zs[(c, nb)]
             zm = work.tile([P, D, 4], BF16, name="zm", tag="zm", bufs=3, align_bytes=64)
             zs[(nb, c)] = zm
-            z32 = z[:].rearrange("p n j -> p (n j)").bitcast(F32).rearrange("p (n w) -> p n w", w=2)
-            for w in range(2):
-                tb = bank([P, 4, P], "tb")
+            for h in range(2):
+                tb = bank([P, 4, 256], "tb", BF16)
                 for j in range(4):
-                    nc.tensor.transpose(tb[:, j, :], z32[:, P * j:P * j + P, w], ident[:])
-                nc.scalar.copy(
-                    out=zm[:, 256 * w:256 * w + 256, :].rearrange("p (e q) j -> p e q j", e=2),
-                    in_=tb[:].bitcast(BF16).rearrange("p j (q e) -> p e q j", e=2),
-                )
+                    for jj in (2 * h, 2 * h + 1):
+                        nc.tensor.transpose(
+                            tb[:, j, P * (jj - 2 * h):P * (jj - 2 * h) + P], z[:, P * j:P * j + P, jj], identb[:]
+                        )
+                nc.scalar.copy(out=zm[:, 256 * h:256 * h + 256, :], in_=tb[:].rearrange("p j n -> p n j"))
 
         def adj_round(g):
             for c in range(g + 1):

@@ -35,23 +35,25 @@ def tile_graphlearner_pa_kernel(tc, feat, mask, W, b, out):
         work = ctx.enter_context(tc.tile_pool(name="work", bufs=2))
         psum = ctx.enter_context(tc.psum_pool(name="psum", bufs=8))
 
-        def bank(shape, name, dtype=F32):
-            return psum.tile(shape, dtype, name=name, tag="ps")
+        banks = {"wide": 6, "turn": 2}
+
+        def bank(shape, name, dtype=F32, tag="wide"):
+            return psum.tile(shape, dtype, name=name, tag=tag, bufs=banks[tag])
 
         def a_offset(c, nb):
             return UPPER.index((c, nb)) * ABLK
 
         mraw = keep.tile([NT, P], BF16, name="mraw")
         nc.sync.dma_start(out=mraw[:], in_=mask_v)
+        fraw = big.tile([P, NT, D], BF16, name="fraw", offset=7 * ABLK)
+        for k in range(4):
+            nc.sync.dma_start(out=fraw[:, 4 * k:4 * k + 4, :], in_=feat_v[:, 4 * k:4 * k + 4, :])
         wraw = big.tile([P, 4, D], BF16, name="wraw", offset=4 * ABLK + 4096)
         for u in range(2):
             nc.sync.dma_start(
                 out=wraw[:, 2 * u:2 * u + 2, :],
                 in_=W[256 * u:256 * u + 256, :].rearrange("(q e) c -> q e c", e=2),
             )
-        fraw = big.tile([P, NT, D], BF16, name="fraw", offset=7 * ABLK)
-        for k in range(4):
-            nc.sync.dma_start(out=fraw[:, 4 * k:4 * k + 4, :], in_=feat_v[:, 4 * k:4 * k + 4, :])
 
         ident = keep.tile([P, P], F32, name="ident")
         make_identity(nc, ident[:])
@@ -64,17 +66,18 @@ def tile_graphlearner_pa_kernel(tc, feat, mask, W, b, out):
         mpad = keep.tile([P, P], F32, name="mpad")
         nc.vector.memset(mpad[:], 0.0)
         nc.vector.tensor_copy(out=mpad[0:NT, :], in_=mraw[:])
-        mps = bank([P, P], "mps")
+        mps = bank([P, P], "mps", tag="turn")
         nc.tensor.transpose(mps[:], mpad[:], ident[:])
         mcol = keep.tile([P, NT], F32, name="mcol")
         nc.vector.tensor_copy(out=mcol[:], in_=mps[:, 0:NT])
         diag = keep.tile([P, NT, P], F32, name="diag")
-        nc.vector.tensor_tensor(
-            out=diag[:],
-            in0=ident[:].unsqueeze(1).to_broadcast([P, NT, P]),
-            in1=mcol[:].unsqueeze(2).to_broadcast([P, NT, P]),
-            op=ALU.mult,
-        )
+        for k in range(4):
+            nc.vector.tensor_tensor(
+                out=diag[:, 4 * k:4 * k + 4, :],
+                in0=ident[:].unsqueeze(1).to_broadcast([P, 4, P]),
+                in1=mcol[:, 4 * k:4 * k + 4].unsqueeze(2).to_broadcast([P, 4, P]),
+                op=ALU.mult,
+            )
 
         xq = keep.tile([P, N], U32, name="xq", align_bytes=64)
         xqs = keep.tile([P, N], U8, name="xqs", align_bytes=64)
@@ -85,60 +88,54 @@ def tile_graphlearner_pa_kernel(tc, feat, mask, W, b, out):
         wq = big.tile([P, D], U32, name="wq", offset=EBASE + 10240, align_bytes=64)
         wqs = big.tile([P, D], U8, name="wqs", offset=EBASE + 12288, align_bytes=64)
 
-        wg = big.tile([P, D, 4], BF16, name="wg", offset=4 * ABLK, align_bytes=64)
-        wv = wraw[:].rearrange("p j (u r e) -> p u e r j", u=2, e=2)
-        for u in range(2):
-            for e in range(2):
-                eb = 2 * u + e
-                nc.vector.tensor_copy(out=wg[:, P * eb:P * eb + P, :], in_=wv[:, u, e])
-        nc.vector.quantize_mx(out=wq[:].bitcast(FP8X4), scales=wqs[:], in_=wg[:].rearrange("p w j -> p (w j)"))
-
         gram = [bank([P, P], "gram%d" % k) for k in range(4)]
+        for t in range(NT):
+            fv = fraw[:, t, :].rearrange("p (u q e) -> p u q e", u=2, e=2)
+            for u in range(2):
+                for e in range(2):
+                    s = fv[:, u, :, e]
+                    nc.tensor.matmul(gram[2 * u + e][:], lhsT=s, rhs=s, start=(t == 0), stop=(t == NT - 1))
+        junk = keep.tile([P, 4, P], F32, name="junk")
+        n2 = keep.tile([P, 4], F32, name="n2")
+        for k in range(4):
+            nc.vector.scalar_tensor_tensor(
+                out=junk[:, k, :], in0=gram[k][:], scalar=1.0, in1=ident[:], op0=ALU.mult, op1=ALU.mult,
+                accum_out=n2[:, k:k + 1],
+            )
+        n2c = keep.tile([P, 4], F32, name="n2c")
+        nc.vector.tensor_scalar_max(out=n2c[:], in0=n2[:], scalar1=1e-24)
+        nrm = keep.tile([P, 4], F32, name="nrm")
+        nc.scalar.sqrt(out=nrm[:], in_=n2c[:])
+        rn = keep.tile([P, 4], F32, name="rn")
+        nc.vector.reciprocal(out=rn[:], in_=nrm[:])
+        rn_b = rn[:].rearrange("p (u e) -> p u e", u=2).unsqueeze(1).to_broadcast([P, 256, 2, 2])
+
         fgs = []
+        for k in range(4):
+            fg = big.tile([P, 4 * D], BF16, name="fg", tag="fg", bufs=4, offset=5 * ABLK, align_bytes=64)
+            fgs.append(fg)
+            fg32 = fg[:].bitcast(F32).rearrange("p (n u) -> p n u", u=2)
+            for hh in range(2):
+                tp = bank([P, 2, 256], "tp", tag="turn" if hh else "wide")
+                for tt in range(2):
+                    t = 4 * k + 2 * hh + tt
+                    f32v = fraw[:, t, :].bitcast(F32)
+                    for u in range(2):
+                        nc.tensor.transpose(tp[:, u, P * tt:P * tt + P], f32v[:, P * u:P * u + P], diag[:, t, :])
+                nc.scalar.copy(out=fg32[:, 256 * hh:256 * hh + 256, :], in_=tp[:].rearrange("p u n -> p n u"))
 
         def quantise_feat(k):
             nc.vector.quantize_mx(
                 out=fq[:, D * k:D * k + D].bitcast(FP8X4), scales=fqs[:, D * k:D * k + D], in_=fgs[k][:]
             )
 
-        for k in range(4):
-            fg = big.tile([P, 4 * D], BF16, name="fg", tag="fg", bufs=4, offset=5 * ABLK, align_bytes=64)
-            fgs.append(fg)
-            fg32 = fg[:].bitcast(F32).rearrange("p (n u) -> p n u", u=2)
-            for t in range(4 * k, 4 * k + 4):
-                fv = fraw[:, t, :].rearrange("p (u q e) -> p u q e", u=2, e=2)
-                for u in range(2):
-                    for e in range(2):
-                        s = fv[:, u, :, e]
-                        nc.tensor.matmul(gram[2 * u + e][:], lhsT=s, rhs=s, start=(t == 0), stop=(t == NT - 1))
-            for hh in range(2):
-                tp = bank([P, 2, 256], "tp")
-                for tt in range(2):
-                    f32v = fraw[:, 4 * k + 2 * hh + tt, :].bitcast(F32)
-                    for u in range(2):
-                        nc.tensor.transpose(tp[:, u, P * tt:P * tt + P], f32v[:, P * u:P * u + P], ident[:])
-                nc.scalar.copy(out=fg32[:, 256 * hh:256 * hh + 256, :], in_=tp[:].rearrange("p u n -> p n u"))
-            if k < 2:
-                quantise_feat(k)
-
-        tms = {}
-
-        def masked_transposes(k):
-            for hh in range(2):
-                tm = bank([P, 2, 256], "tm")
-                tms[2 * k + hh] = tm
-                for tt in range(2):
-                    t = 4 * k + 2 * hh + tt
-                    f32v = fraw[:, t, :].bitcast(F32)
-                    for u in range(2):
-                        nc.tensor.transpose(tm[:, u, P * tt:P * tt + P], f32v[:, P * u:P * u + P], diag[:, t, :])
-
         pgs = {}
 
-        def pre_sup(c, engine):
-            pg = big.tile([P, D, 4], BF16, name="pg", tag="pg", bufs=4, offset=EBASE + 13312, align_bytes=64)
-            pgs[c] = pg
-            for eb in range(4):
+        def pre_sup(c, engine, ebs=range(4)):
+            if c not in pgs:
+                pgs[c] = big.tile([P, D, 4], BF16, name="pg", tag="pg", bufs=4, offset=EBASE + 13312, align_bytes=64)
+            pg = pgs[c]
+            for eb in ebs:
                 pp = bank([P, 4, P], "pp")
                 for j in range(4):
                     i = 4 * c + j
@@ -165,6 +162,8 @@ def tile_graphlearner_pa_kernel(tc, feat, mask, W, b, out):
         five = keep.tile([P, 5], F32, name="five")
         dcol = keep.tile([P, NT], F32, name="dcol")
         dbc = keep.tile([P, N], F32, name="dbc")
+        shared = {(0, 3): (1, 3), (1, 3): (1, 3), (1, 2): (1, 3), (2, 0): (3,), (2, 1): (3,), (2, 3): (3,)}
+        rowengine = {(3, 3): "S"}
         A = {}
         aq = {}
         aqs = {}
@@ -187,37 +186,23 @@ def tile_graphlearner_pa_kernel(tc, feat, mask, W, b, out):
                 if nb >= c:
                     row = A[(c, nb)][:, j, :]
                 else:
-                    unused = work.tile([P, D], BF16, name="unused", tag="unused")
+                    unused = work.tile([P, D], BF16, name="unused", tag="unused", bufs=4)
                     row = unused[:]
-                nc.scalar.activation(out=row, in_=ep[:], func=ACT.Relu, accum_out=degs[:, i, nb:nb + 1])
+                if j in shared.get((c, nb), ()):
+                    nc.vector.tensor_scalar(
+                        out=row, in0=ep[:], scalar1=0.0, scalar2=None, op0=ALU.max, op1=ALU.add,
+                        accum_out=degs[:, i, nb:nb + 1],
+                    )
+                else:
+                    nc.scalar.activation(out=row, in_=ep[:], func=ACT.Relu, accum_out=degs[:, i, nb:nb + 1])
+            if nb == c:
+                for j in range(4):
+                    blk = A[(c, c)][:, j, P * j:P * j + P]
+                    nc.gpsimd.tensor_tensor(out=blk, in0=blk, in1=diag[:, 4 * c + j, :], op=ALU.add)
 
-        def self_loops(c):
-            for j in range(4):
-                blk = A[(c, c)][:, j, P * j:P * j + P]
-                nc.vector.tensor_tensor(out=blk, in0=blk, in1=diag[:, 4 * c + j, :], op=ALU.add)
-
-        def edge_round(c, part=slice(0, 4)):
-            for nb in ([c] + [x for x in range(4) if x != c])[part]:
+        def edge_round(c, chosen=slice(0, 4)):
+            for nb in ([c] + [x for x in range(4) if x != c])[chosen]:
                 edge_unit(c, nb)
-
-        masked_transposes(0)
-        masked_transposes(1)
-        junk = keep.tile([P, P], F32, name="junk")
-        n2 = keep.tile([P, 4], F32, name="n2")
-        for k in range(4):
-            nc.vector.scalar_tensor_tensor(
-                out=junk[:], in0=gram[k][:], scalar=1.0, in1=ident[:], op0=ALU.mult, op1=ALU.mult,
-                accum_out=n2[:, k:k + 1],
-            )
-        n2c = keep.tile([P, 4], F32, name="n2c")
-        nc.vector.tensor_scalar_max(out=n2c[:], in0=n2[:], scalar1=1e-24)
-        nrm = keep.tile([P, 4], F32, name="nrm")
-        nc.scalar.sqrt(out=nrm[:], in_=n2c[:])
-        rn = keep.tile([P, 4], F32, name="rn")
-        nc.vector.reciprocal(out=rn[:], in_=nrm[:])
-        rn_b = rn[:].rearrange("p (u e) -> p u e", u=2).unsqueeze(1).to_broadcast([P, 256, 2, 2])
-        pre_sup(0, nc.scalar.copy)
-        pre_sup(1, nc.scalar.copy)
 
         xgs = {}
 
@@ -225,65 +210,57 @@ def tile_graphlearner_pa_kernel(tc, feat, mask, W, b, out):
             k, hh = divmod(h, 2)
             if hh == 0:
                 xgs[k] = big.tile([P, 4 * D], BF16, name="xg", tag="xg", bufs=2, offset=9 * ABLK, align_bytes=64)
-            xgv = xgs[k][:].rearrange("p (n u e) -> p n u e", u=2, e=2)
+            half = slice(1024 * hh, 1024 * hh + 1024)
             nc.vector.tensor_tensor(
-                out=xgv[:, 256 * hh:256 * hh + 256],
-                in0=tms[h][:].bitcast(BF16).rearrange("p u (n e) -> p n u e", e=2),
+                out=xgs[k][:, half].rearrange("p (n u e) -> p n u e", u=2, e=2),
+                in0=fgs[k][:, half].rearrange("p (n u e) -> p n u e", u=2, e=2),
                 in1=rn_b,
                 op=ALU.mult,
             )
 
-        def quantise_xn(k):
+        def quantise_xn(h):
+            k, hh = divmod(h, 2)
+            cols = slice(256 * h, 256 * h + 256)
             nc.vector.quantize_mx(
-                out=xq[:, D * k:D * k + D].bitcast(FP8X4), scales=xqs[:, D * k:D * k + D], in_=xgs[k][:]
+                out=xq[:, cols].bitcast(FP8X4), scales=xqs[:, cols], in_=xgs[k][:, 1024 * hh:1024 * hh + 1024]
             )
 
-        scale_xn(0)
-        scale_xn(1)
-        masked_transposes(2)
-        scale_xn(2)
-        quantise_xn(0)
-        edge_unit(0, 0)
-        scale_xn(3)
-        masked_transposes(3)
-        scale_xn(4)
-        quantise_xn(1)
-        edge_unit(0, 1)
-        scale_xn(5)
-        scale_xn(6)
-        quantise_xn(2)
-        edge_unit(0, 2)
-        scale_xn(7)
-        quantise_xn(3)
-        edge_unit(0, 3)
-        quantise_feat(2)
-        quantise_feat(3)
-        quantise_pre_sup(0)
-        pre_sup(2, nc.vector.tensor_copy)
-        quantise_pre_sup(1)
-        pre_sup(3, nc.vector.tensor_copy)
-        quantise_pre_sup(2)
+        def weights():
+            wg = big.tile([P, D, 4], BF16, name="wg", offset=4 * ABLK, align_bytes=64)
+            wv = wraw[:].rearrange("p j (u r e) -> p u e r j", u=2, e=2)
+            for u in range(2):
+                for e in range(2):
+                    eb = 2 * u + e
+                    nc.gpsimd.tensor_scalar(
+                        out=wg[:, P * eb:P * eb + P, :], in0=wv[:, u, e], scalar1=1.0, scalar2=0.0, op0=ALU.mult, op1=ALU.add
+                    )
+            nc.vector.quantize_mx(out=wq[:].bitcast(FP8X4), scales=wqs[:], in_=wg[:].rearrange("p w j -> p (w j)"))
 
         def degrees(g):
             for i in range(4 * g, 4 * g + 4):
                 nc.scalar.activation(out=five[:], in_=degs[:, i, :], func=ACT.Copy, accum_out=deg[:, i:i + 1])
             nc.scalar.sqrt(out=sdeg[:, 4 * g:4 * g + 4], in_=deg[:, 4 * g:4 * g + 4])
 
-        def spread(g, meanwhile=()):
-            nc.vector.reciprocal(out=dcol[:, 4 * g:4 * g + 4], in_=sdeg[:, 4 * g:4 * g + 4])
-            rep = work.tile([P, 4, P], F32, name="rep", tag="rep")
-            nc.vector.tensor_copy(out=rep[:], in_=dcol[:, 4 * g:4 * g + 4].unsqueeze(2).to_broadcast([P, 4, P]))
-            dp = bank([P, D], "dp")
+        def spread(g):
+            cols = slice(4 * g, 4 * g + 4)
+            nc.vector.reciprocal(out=dcol[:, cols], in_=sdeg[:, cols])
+            dp = bank([P, D], "dp", tag="turn")
             for j in range(4):
-                nc.tensor.transpose(dp[:, P * j:P * j + P], rep[:, j, :], ident[:])
-            self_loops(g)
-            for nb in range(g, 4):
-                for j in range(4):
-                    row = A[(g, nb)][:, j, :]
-                    nc.vector.tensor_scalar_mul(out=row, in0=row, scalar1=dcol[:, 4 * g + j:4 * g + j + 1])
-            for job in meanwhile:
-                job()
+                nc.tensor.transpose(
+                    dp[:, P * j:P * j + P], dcol[:, 4 * g + j:4 * g + j + 1].to_broadcast([P, P]), ident[:]
+                )
             nc.vector.tensor_copy(out=dbc[:, D * g:D * g + D], in_=dp[:])
+        def scale_rows(c, nb):
+            for j in range(4):
+                row = A[(c, nb)][:, j, :]
+                d = dcol[:, 4 * c + j:4 * c + j + 1]
+                who = rowengine.get((c, nb), "V")
+                if who == "G":
+                    nc.gpsimd.tensor_scalar(out=row, in0=row, scalar1=d, scalar2=0.0, op0=ALU.mult, op1=ALU.add)
+                elif who == "S":
+                    nc.scalar.activation(out=row, in_=row, func=ACT.Copy, scale=d)
+                else:
+                    nc.vector.tensor_scalar_mul(out=row, in0=row, scalar1=d)
 
         zs = {}
 
@@ -301,7 +278,7 @@ def tile_graphlearner_pa_kernel(tc, feat, mask, W, b, out):
                 in_=zs[(c, nb)][:].rearrange("p n j -> p (n j)"),
             )
 
-        def scale_columns(c, nb):
+        def scale(c, nb):
             z = work.tile([P, D, 4], BF16, name="z", tag="z", bufs=4, align_bytes=64)
             zs[(c, nb)] = z
             nc.vector.tensor_tensor(
@@ -311,12 +288,13 @@ def tile_graphlearner_pa_kernel(tc, feat, mask, W, b, out):
                 op=ALU.mult,
             )
 
-        def mirror(c, nb):
+        def mirror(c, nb, halves=range(2)):
             z = zs[(c, nb)]
-            zm = work.tile([P, D, 4], BF16, name="zm", tag="zm", bufs=3, align_bytes=64)
-            zs[(nb, c)] = zm
-            for h in range(2):
-                tb = bank([P, 4, 256], "tb", BF16)
+            if (nb, c) not in zs:
+                zs[(nb, c)] = work.tile([P, D, 4], BF16, name="zm", tag="zm", bufs=3, align_bytes=64)
+            zm = zs[(nb, c)]
+            for h in halves:
+                tb = bank([P, 4, 256], "tb", BF16, tag="turn")
                 for j in range(4):
                     for jj in (2 * h, 2 * h + 1):
                         nc.tensor.transpose(
@@ -324,56 +302,36 @@ def tile_graphlearner_pa_kernel(tc, feat, mask, W, b, out):
                         )
                 nc.scalar.copy(out=zm[:, 256 * h:256 * h + 256, :], in_=tb[:].rearrange("p j n -> p n j"))
 
-        def adj_round(g):
-            for c in range(g + 1):
-                scale_columns(c, g)
-                if c < g:
-                    mirror(c, g)
-                if c > 0:
-                    quantise(c - 1, g)
-            quantise(g, g)
-
-        def mirrors_of(g):
-            for c in range(g):
-                quantise(g, c)
-
-        degrees(0)
-        edge_round(1)
-        degrees(1)
-        quantise_pre_sup(3)
-        spread(0)
-        edge_round(2, slice(0, 2))
-        adj_round(0)
-        spread(1)
-        edge_round(2, slice(2, 4))
-        degrees(2)
-        edge_round(3, slice(0, 2))
-        adj_round(1)
-        spread(2)
-        edge_round(3, slice(2, 4))
-        degrees(3)
-        adj_round(2)
-        spread(3, [lambda: mirrors_of(1), lambda: mirrors_of(2)])
+        def block(c, nb):
+            scale(c, nb)
+            if c < nb:
+                mirror(c, nb)
+            quantise(c, nb)
+            if c < nb:
+                quantise(nb, c)
 
         bT = keep.tile([P, 2, 2 * N], BF16, name="bT")
+
+        braws = [big.tile([P, 4, D], BF16, name="braw%d" % k, offset=2 * ABLK + 4096 * k) for k in range(4)]
+
+        def bias(k, u):
+            bp = bank([P, D], "bp", tag="turn")
+            for tt in range(4):
+                nc.tensor.transpose(
+                    bp[:, P * tt:P * tt + P], braws[k][:, tt, :].bitcast(F32)[:, P * u:P * u + P], diag[:, 4 * k + tt, :]
+                )
+            nc.scalar.copy(out=bT[:, u, 2 * D * k:2 * D * k + 2 * D], in_=bp[:].bitcast(BF16))
+
         for k in range(4):
-            braw = big.tile([P, 4, D], BF16, name="braw%d" % k, offset=EBASE + 4096 * k)
-            nc.sync.dma_start(out=braw[:], in_=b_v[:, 4 * k:4 * k + 4, :])
-            for u in range(2):
-                bp = bank([P, D], "bp")
-                for tt in range(4):
-                    nc.tensor.transpose(
-                        bp[:, P * tt:P * tt + P], braw[:, tt, :].bitcast(F32)[:, P * u:P * u + P], diag[:, 4 * k + tt, :]
-                    )
-                nc.scalar.copy(out=bT[:, u, 2 * D * k:2 * D * k + 2 * D], in_=bp[:].bitcast(BF16))
+            nc.sync.dma_start(out=braws[k][:], in_=b_v[:, 4 * k:4 * k + 4, :])
 
         acc = {}
 
-        def passes(nb, cs):
+        def passes(nb, cs, tag="wide"):
             for c in cs:
                 for et in range(4):
-                    if c == 0:
-                        acc[(nb, et)] = bank([P, D], "acc")
+                    if (nb, et) not in acc:
+                        acc[(nb, et)] = bank([P, D], "acc", tag=tag if tag == "wide" else "wide")
                     nc.tensor.matmul_mx(
                         out=acc[(nb, et)][:],
                         lhsT=pq[:, c, P * et:P * et + P].bitcast(FP8X4),
@@ -393,26 +351,85 @@ def tile_graphlearner_pa_kernel(tc, feat, mask, W, b, out):
                     nc.scalar.activation(out=y[:], in_=y[:], func=ACT.Tanh)
                     nc.sync.dma_start(out=out_v[u, e][:, D * nb:D * nb + D], in_=y[:])
 
+        weights()
+        for k in range(4):
+            bias(k, 0)
+            bias(k, 1)
+        for k in range(4):
+            scale_xn(2 * k)
+            scale_xn(2 * k + 1)
+            quantise_xn(2 * k)
+            quantise_xn(2 * k + 1)
+            edge_unit(0, k)
+        for k in range(4):
+            quantise_feat(k)
+        degrees(0)
+        spread(0)
+        edge_round(1)
+        degrees(1)
+        for nb in range(3):
+            scale_rows(0, nb)
+        spread(1)
+        pre_sup(0, nc.scalar.copy)
+        quantise_pre_sup(0)
+        edge_round(2, slice(0, 2))
+        scale(0, 0)
+        scale_rows(1, 1)
+        scale_rows(1, 2)
+        scale(0, 1)
+        mirror(0, 1)
+        quantise(0, 0)
+        pre_sup(1, nc.scalar.copy)
+        edge_round(2, slice(2, 4))
+        degrees(2)
+        spread(2)
+        scale(1, 1)
+        quantise_pre_sup(1)
+        quantise(0, 1)
+        quantise(1, 0)
+        edge_round(3)
+        degrees(3)
+        spread(3)
+        quantise(1, 1)
+        scale_rows(0, 3)
+        scale_rows(2, 2)
+        scale(0, 2)
+        mirror(0, 2)
+        pre_sup(2, nc.scalar.copy)
+        scale_rows(1, 3)
+        quantise_pre_sup(2)
+        pre_sup(3, nc.scalar.copy)
+        scale_rows(2, 3)
+        quantise_pre_sup(3)
+        scale_rows(3, 3)
+        quantise(0, 2)
+        quantise(2, 0)
         passes(0, range(3))
-        scale_columns(0, 3)
+        scale(0, 3)
         mirror(0, 3)
-        scale_columns(1, 3)
-        mirror(1, 3)
+        scale(1, 2)
         quantise(0, 3)
-        scale_columns(2, 3)
-        mirror(2, 3)
-        quantise(1, 3)
         quantise(3, 0)
+        mirror(1, 2)
         passes(0, [3])
-        scale_columns(3, 3)
-        quantise(2, 3)
+        scale(1, 3)
+        mirror(1, 3)
+        quantise(1, 2)
+        quantise(2, 1)
+        finish(0)
+        scale(2, 2)
+        quantise(1, 3)
         quantise(3, 1)
         passes(1, range(4))
-        quantise(3, 3)
-        finish(0)
-        passes(3, range(4))
-        quantise(3, 2)
+        scale(2, 3)
+        mirror(2, 3)
+        quantise(2, 2)
         finish(1)
+        scale(3, 3)
+        quantise(2, 3)
+        quantise(3, 2)
         passes(2, range(4))
-        finish(3)
+        quantise(3, 3)
+        passes(3, range(4))
         finish(2)
+        finish(3)

@@ -198,7 +198,7 @@ def tile_graphlearner_pa_kernel(tc, feat, mask, W, b, out):
             if nb == c:
                 for j in range(4):
                     blk = A[(c, c)][:, j, P * j:P * j + P]
-                    nc.gpsimd.tensor_tensor(out=blk, in0=blk, in1=diag[:, 4 * c + j, :], op=ALU.add)
+                    nc.vector.tensor_tensor(out=blk, in0=blk, in1=diag[:, 4 * c + j, :], op=ALU.add)
 
         def edge_round(c, chosen=slice(0, 4)):
             for nb in ([c] + [x for x in range(4) if x != c])[chosen]:
@@ -231,9 +231,7 @@ def tile_graphlearner_pa_kernel(tc, feat, mask, W, b, out):
             for u in range(2):
                 for e in range(2):
                     eb = 2 * u + e
-                    nc.gpsimd.tensor_scalar(
-                        out=wg[:, P * eb:P * eb + P, :], in0=wv[:, u, e], scalar1=1.0, scalar2=0.0, op0=ALU.mult, op1=ALU.add
-                    )
+                    nc.vector.tensor_copy(out=wg[:, P * eb:P * eb + P, :], in_=wv[:, u, e])
             nc.vector.quantize_mx(out=wq[:].bitcast(FP8X4), scales=wqs[:], in_=wg[:].rearrange("p w j -> p (w j)"))
 
         def degrees(g):

@@ -30,6 +30,7 @@ def tile_graphlearner_pa_kernel(tc, feat, mask, W, b, out):
     out_v = out.flatten_outer_dims().rearrange("(u r e) n -> u e r n", u=2, e=2)
 
     with ExitStack() as ctx:
+        ctx.enter_context(tc.manual_schedule())
         big = ctx.enter_context(tc.tile_pool(name="big", bufs=1))
         keep = ctx.enter_context(tc.tile_pool(name="keep", bufs=1))
         work = ctx.enter_context(tc.tile_pool(name="work", bufs=2))
@@ -88,30 +89,18 @@ def tile_graphlearner_pa_kernel(tc, feat, mask, W, b, out):
         wq = big.tile([P, D], U32, name="wq", offset=EBASE + 10240, align_bytes=64)
         wqs = big.tile([P, D], U8, name="wqs", offset=EBASE + 12288, align_bytes=64)
 
-        gram = [bank([P, P], "gram%d" % k) for k in range(4)]
-        for t in range(NT):
-            fv = fraw[:, t, :].rearrange("p (u q e) -> p u q e", u=2, e=2)
-            for u in range(2):
-                for e in range(2):
-                    s = fv[:, u, :, e]
-                    nc.tensor.matmul(gram[2 * u + e][:], lhsT=s, rhs=s, start=(t == 0), stop=(t == NT - 1))
-        junk = keep.tile([P, 4, P], F32, name="junk")
-        n2 = keep.tile([P, 4], F32, name="n2")
-        for k in range(4):
-            nc.vector.scalar_tensor_tensor(
-                out=junk[:, k, :], in0=gram[k][:], scalar=1.0, in1=ident[:], op0=ALU.mult, op1=ALU.mult,
-                accum_out=n2[:, k:k + 1],
-            )
-        n2c = keep.tile([P, 4], F32, name="n2c")
-        nc.vector.tensor_scalar_max(out=n2c[:], in0=n2[:], scalar1=1e-24)
-        nrm = keep.tile([P, 4], F32, name="nrm")
-        nc.scalar.sqrt(out=nrm[:], in_=n2c[:])
-        rn = keep.tile([P, 4], F32, name="rn")
-        nc.vector.reciprocal(out=rn[:], in_=nrm[:])
-        rn_b = rn[:].rearrange("p (u e) -> p u e", u=2).unsqueeze(1).to_broadcast([P, 256, 2, 2])
-
+        gram = [bank([P, P], "gram%d" % k, tag="wide") for k in range(4)]
         fgs = []
-        for k in range(4):
+
+        def gram_of(k):
+            for t in range(4 * k, 4 * k + 4):
+                fv = fraw[:, t, :].rearrange("p (u q e) -> p u q e", u=2, e=2)
+                for u in range(2):
+                    for e in range(2):
+                        s = fv[:, u, :, e]
+                        nc.tensor.matmul(gram[2 * u + e][:], lhsT=s, rhs=s, start=(t == 0), stop=(t == NT - 1))
+
+        def turn_feat(k):
             fg = big.tile([P, 4 * D], BF16, name="fg", tag="fg", bufs=4, offset=5 * ABLK, align_bytes=64)
             fgs.append(fg)
             fg32 = fg[:].bitcast(F32).rearrange("p (n u) -> p n u", u=2)
@@ -123,6 +112,22 @@ def tile_graphlearner_pa_kernel(tc, feat, mask, W, b, out):
                     for u in range(2):
                         nc.tensor.transpose(tp[:, u, P * tt:P * tt + P], f32v[:, P * u:P * u + P], diag[:, t, :])
                 nc.scalar.copy(out=fg32[:, 256 * hh:256 * hh + 256, :], in_=tp[:].rearrange("p u n -> p n u"))
+
+        junk = keep.tile([P, 4, P], F32, name="junk")
+        n2 = keep.tile([P, 4], F32, name="n2")
+        n2c = keep.tile([P, 4], F32, name="n2c")
+        nrm = keep.tile([P, 4], F32, name="nrm")
+        rn = keep.tile([P, 4], F32, name="rn")
+        rn_b = rn[:].rearrange("p (u e) -> p u e", u=2).unsqueeze(1).to_broadcast([P, 256, 2, 2])
+
+        def norm_sums():
+            for k in range(4):
+                nc.vector.scalar_tensor_tensor(
+                    out=junk[:, k, :], in0=gram[k][:], scalar=1.0, in1=ident[:], op0=ALU.mult, op1=ALU.mult,
+                    accum_out=n2[:, k:k + 1],
+                )
+            nc.vector.tensor_scalar_max(out=n2c[:], in0=n2[:], scalar1=1e-24)
+            nc.scalar.sqrt(out=nrm[:], in_=n2c[:])
 
         def quantise_feat(k):
             nc.vector.quantize_mx(
@@ -162,16 +167,15 @@ def tile_graphlearner_pa_kernel(tc, feat, mask, W, b, out):
         five = keep.tile([P, 5], F32, name="five")
         dcol = keep.tile([P, NT], F32, name="dcol")
         dbc = keep.tile([P, N], F32, name="dbc")
-        shared = {(0, 3): (1, 3), (1, 3): (1, 3), (1, 2): (1, 3), (2, 0): (3,), (2, 1): (3,), (2, 3): (3,)}
         rowengine = {(3, 3): "S"}
         A = {}
         aq = {}
         aqs = {}
 
-        def edge_unit(c, nb):
-            if nb >= c:
+        def edge_unit(c, nb, js=range(4), vec=()):
+            if nb >= c and (c, nb) not in A:
                 A[(c, nb)] = big.tile([P, 4, D], F32, name="A%d_%d" % (c, nb), offset=a_offset(c, nb))
-            for j in range(4):
+            for j in js:
                 i = 4 * c + j
                 ep = bank([P, D], "ep")
                 nc.tensor.matmul_mx(
@@ -188,21 +192,19 @@ def tile_graphlearner_pa_kernel(tc, feat, mask, W, b, out):
                 else:
                     unused = work.tile([P, D], BF16, name="unused", tag="unused", bufs=4)
                     row = unused[:]
-                if j in shared.get((c, nb), ()):
+                if j in vec:
                     nc.vector.tensor_scalar(
                         out=row, in0=ep[:], scalar1=0.0, scalar2=None, op0=ALU.max, op1=ALU.add,
                         accum_out=degs[:, i, nb:nb + 1],
                     )
                 else:
                     nc.scalar.activation(out=row, in_=ep[:], func=ACT.Relu, accum_out=degs[:, i, nb:nb + 1])
-            if nb == c:
+
+        def self_loops(c):
                 for j in range(4):
                     blk = A[(c, c)][:, j, P * j:P * j + P]
                     nc.vector.tensor_tensor(out=blk, in0=blk, in1=diag[:, 4 * c + j, :], op=ALU.add)
 
-        def edge_round(c, chosen=slice(0, 4)):
-            for nb in ([c] + [x for x in range(4) if x != c])[chosen]:
-                edge_unit(c, nb)
 
         xgs = {}
 
@@ -225,13 +227,16 @@ def tile_graphlearner_pa_kernel(tc, feat, mask, W, b, out):
                 out=xq[:, cols].bitcast(FP8X4), scales=xqs[:, cols], in_=xgs[k][:, 1024 * hh:1024 * hh + 1024]
             )
 
+        wg = big.tile([P, D, 4], BF16, name="wg", offset=4 * ABLK, align_bytes=64)
+
         def weights():
-            wg = big.tile([P, D, 4], BF16, name="wg", offset=4 * ABLK, align_bytes=64)
             wv = wraw[:].rearrange("p j (u r e) -> p u e r j", u=2, e=2)
             for u in range(2):
                 for e in range(2):
                     eb = 2 * u + e
                     nc.vector.tensor_copy(out=wg[:, P * eb:P * eb + P, :], in_=wv[:, u, e])
+
+        def quantise_weights():
             nc.vector.quantize_mx(out=wq[:].bitcast(FP8X4), scales=wqs[:], in_=wg[:].rearrange("p w j -> p (w j)"))
 
         def degrees(g):
@@ -239,23 +244,29 @@ def tile_graphlearner_pa_kernel(tc, feat, mask, W, b, out):
                 nc.scalar.activation(out=five[:], in_=degs[:, i, :], func=ACT.Copy, accum_out=deg[:, i:i + 1])
             nc.scalar.sqrt(out=sdeg[:, 4 * g:4 * g + 4], in_=deg[:, 4 * g:4 * g + 4])
 
-        def spread(g):
+        def d_of(g):
             cols = slice(4 * g, 4 * g + 4)
             nc.vector.reciprocal(out=dcol[:, cols], in_=sdeg[:, cols])
+
+        dps = {}
+
+        def spread_d(g):
             dp = bank([P, D], "dp", tag="turn")
+            dps[g] = dp
             for j in range(4):
                 nc.tensor.transpose(
                     dp[:, P * j:P * j + P], dcol[:, 4 * g + j:4 * g + j + 1].to_broadcast([P, P]), ident[:]
                 )
-            nc.vector.tensor_copy(out=dbc[:, D * g:D * g + D], in_=dp[:])
+
+        def keep_d(g):
+            nc.vector.tensor_copy(out=dbc[:, D * g:D * g + D], in_=dps[g][:])
+
         def scale_rows(c, nb):
             for j in range(4):
                 row = A[(c, nb)][:, j, :]
                 d = dcol[:, 4 * c + j:4 * c + j + 1]
                 who = rowengine.get((c, nb), "V")
-                if who == "G":
-                    nc.gpsimd.tensor_scalar(out=row, in0=row, scalar1=d, scalar2=0.0, op0=ALU.mult, op1=ALU.add)
-                elif who == "S":
+                if who == "S":
                     nc.scalar.activation(out=row, in_=row, func=ACT.Copy, scale=d)
                 else:
                     nc.vector.tensor_scalar_mul(out=row, in0=row, scalar1=d)
@@ -310,7 +321,7 @@ def tile_graphlearner_pa_kernel(tc, feat, mask, W, b, out):
 
         bT = keep.tile([P, 2, 2 * N], BF16, name="bT")
 
-        braws = [big.tile([P, 4, D], BF16, name="braw%d" % k, offset=2 * ABLK + 4096 * k) for k in range(4)]
+        braws = [big.tile([P, 4, D], BF16, name="braw%d" % k, offset=EBASE + 29696 + 4096 * k) for k in range(4)]
 
         def bias(k, u):
             bp = bank([P, D], "bp", tag="turn")
@@ -324,110 +335,167 @@ def tile_graphlearner_pa_kernel(tc, feat, mask, W, b, out):
             nc.sync.dma_start(out=braws[k][:], in_=b_v[:, 4 * k:4 * k + 4, :])
 
         acc = {}
+        done = {}
 
-        def passes(nb, cs, tag="wide"):
+        def passes(nb, cs, ets=range(4), tag="wide"):
             for c in cs:
-                for et in range(4):
-                    if (nb, et) not in acc:
-                        acc[(nb, et)] = bank([P, D], "acc", tag=tag if tag == "wide" else "wide")
+                for et in ets:
+                    first = (nb, et) not in acc
+                    if first:
+                        acc[(nb, et)] = bank([P, D], "acc", tag=tag)
+                        done[(nb, et)] = 0
+                    done[(nb, et)] += 1
                     nc.tensor.matmul_mx(
                         out=acc[(nb, et)][:],
                         lhsT=pq[:, c, P * et:P * et + P].bitcast(FP8X4),
                         lhsT_scale=pqs[:, c, P * et:P * et + P],
                         rhs=aq[(c, nb)][:].bitcast(FP8X4),
                         rhs_scale=aqs[(c, nb)][:],
-                        start=(c == 0),
-                        stop=(c == 3),
+                        start=first,
+                        stop=(done[(nb, et)] == 4),
                     )
 
         def finish(nb):
             for u in range(2):
                 for e in range(2):
-                    y = work.tile([P, D], F32, name="y", tag="y", bufs=8)
+                    y = big.tile([P, D], F32, name="y", tag="y", bufs=8, offset=EBASE + 29696)
                     bview = bT[:, u, 2 * D * nb:2 * D * nb + 2 * D].rearrange("p (n e) -> p n e", e=2)
                     nc.vector.tensor_tensor(out=y[:], in0=acc[(nb, 2 * u + e)][:], in1=bview[:, :, e], op=ALU.add)
                     nc.scalar.activation(out=y[:], in_=y[:], func=ACT.Tanh)
                     nc.sync.dma_start(out=out_v[u, e][:, D * nb:D * nb + D], in_=y[:])
 
+
+        gram_of(0)
+        turn_feat(0)
+        gram_of(1)
+        turn_feat(1)
+        gram_of(2)
+        gram_of(3)
+        turn_feat(2)
+        quantise_feat(0)
         weights()
-        for k in range(4):
-            bias(k, 0)
-            bias(k, 1)
-        for k in range(4):
+        quantise_feat(1)
+        quantise_weights()
+        norm_sums()
+        nc.vector.reciprocal(out=rn[:], in_=nrm[:])
+        turn_feat(3)
+        pre_sup(0, nc.scalar.copy)
+        for k in range(2):
             scale_xn(2 * k)
             scale_xn(2 * k + 1)
             quantise_xn(2 * k)
             quantise_xn(2 * k + 1)
-            edge_unit(0, k)
-        for k in range(4):
-            quantise_feat(k)
+        edge_unit(0, 0)
+        edge_unit(1, 0)
+        edge_unit(0, 1)
+        scale_xn(4)
+        scale_xn(5)
+        quantise_xn(4)
+        quantise_xn(5)
+        edge_unit(0, 2)
+        scale_xn(6)
+        scale_xn(7)
+        quantise_xn(6)
+        quantise_xn(7)
+        edge_unit(0, 3, range(4), (1, 3))
+        quantise_feat(2)
         degrees(0)
-        spread(0)
-        edge_round(1)
+        edge_unit(1, 1, range(4), (1, 3))
+        self_loops(0)
+        edge_unit(1, 2)
+        d_of(0)
+        quantise_feat(3)
+        edge_unit(1, 3)
+        self_loops(1)
         degrees(1)
-        for nb in range(3):
-            scale_rows(0, nb)
-        spread(1)
-        pre_sup(0, nc.scalar.copy)
-        quantise_pre_sup(0)
-        edge_round(2, slice(0, 2))
+        spread_d(0)
+        scale_rows(0, 0)
+        pre_sup(1, nc.scalar.copy, [0, 1])
+        edge_unit(2, 2)
+        keep_d(0)
+        scale_rows(0, 1)
+        d_of(1)
         scale(0, 0)
+        edge_unit(2, 0)
         scale_rows(1, 1)
-        scale_rows(1, 2)
+        spread_d(1)
+        edge_unit(2, 1)
+        scale_rows(0, 2)
+        keep_d(1)
         scale(0, 1)
-        mirror(0, 1)
         quantise(0, 0)
-        pre_sup(1, nc.scalar.copy)
-        edge_round(2, slice(2, 4))
+        pre_sup(1, nc.scalar.copy, [2, 3])
+        edge_unit(2, 3)
         degrees(2)
-        spread(2)
         scale(1, 1)
-        quantise_pre_sup(1)
         quantise(0, 1)
-        quantise(1, 0)
-        edge_round(3)
-        degrees(3)
-        spread(3)
-        quantise(1, 1)
+        mirror(0, 1)
+        edge_unit(3, 3)
         scale_rows(0, 3)
+        scale_rows(1, 2)
+        self_loops(2)
+        d_of(2)
+        quantise(1, 1)
+        edge_unit(3, 0)
         scale_rows(2, 2)
-        scale(0, 2)
-        mirror(0, 2)
-        pre_sup(2, nc.scalar.copy)
+        quantise_pre_sup(0)
+        spread_d(2)
+        edge_unit(3, 1)
+        quantise(1, 0)
+        keep_d(2)
         scale_rows(1, 3)
-        quantise_pre_sup(2)
+        scale(0, 2)
+        edge_unit(3, 2)
+        scale(1, 2)
+        quantise_pre_sup(1)
+        mirror(0, 2)
+        quantise(0, 2)
+        degrees(3)
+        mirror(1, 2)
+        self_loops(3)
+        d_of(3)
+        quantise(1, 2)
+        quantise(2, 0)
+        pre_sup(2, nc.scalar.copy)
+        spread_d(3)
+        quantise(2, 1)
+        keep_d(3)
         pre_sup(3, nc.scalar.copy)
         scale_rows(2, 3)
-        quantise_pre_sup(3)
-        scale_rows(3, 3)
-        quantise(0, 2)
-        quantise(2, 0)
-        passes(0, range(3))
+        bias(2, 0)
+        bias(2, 1)
+        quantise_pre_sup(2)
         scale(0, 3)
-        mirror(0, 3)
-        scale(1, 2)
-        quantise(0, 3)
-        quantise(3, 0)
-        mirror(1, 2)
-        passes(0, [3])
         scale(1, 3)
+        quantise_pre_sup(3)
+        passes(0, range(3))
+        mirror(0, 3)
         mirror(1, 3)
-        quantise(1, 2)
-        quantise(2, 1)
-        finish(0)
-        scale(2, 2)
-        quantise(1, 3)
-        quantise(3, 1)
-        passes(1, range(4))
+        bias(0, 0)
         scale(2, 3)
+        quantise(3, 0)
+        scale(2, 2)
+        bias(0, 1)
+        bias(1, 0)
+        bias(1, 1)
+        scale_rows(3, 3)
+        quantise(3, 1)
+        passes(0, [3])
         mirror(2, 3)
+        passes(1, range(4), range(2))
         quantise(2, 2)
-        finish(1)
+        finish(0)
+        passes(1, range(4), range(2, 4))
         scale(3, 3)
-        quantise(2, 3)
+        bias(3, 0)
+        bias(3, 1)
         quantise(3, 2)
+        finish(1)
+        quantise(0, 3)
+        quantise(1, 3)
         passes(2, range(4))
+        quantise(2, 3)
         quantise(3, 3)
-        passes(3, range(4))
         finish(2)
+        passes(3, range(4))
         finish(3)

@@ -36,7 +36,7 @@ def tile_graphlearner_pa_kernel(tc, feat, mask, W, b, out):
         work = ctx.enter_context(tc.tile_pool(name="work", bufs=2))
         psum = ctx.enter_context(tc.psum_pool(name="psum", bufs=8))
 
-        banks = {"wide": 6, "turn": 2}
+        banks = {"wide": 8}
 
         def bank(shape, name, dtype=F32, tag="wide"):
             return psum.tile(shape, dtype, name=name, tag=tag, bufs=banks[tag])
@@ -67,7 +67,7 @@ def tile_graphlearner_pa_kernel(tc, feat, mask, W, b, out):
         mpad = keep.tile([P, P], F32, name="mpad")
         nc.vector.memset(mpad[:], 0.0)
         nc.vector.tensor_copy(out=mpad[0:NT, :], in_=mraw[:])
-        mps = bank([P, P], "mps", tag="turn")
+        mps = bank([P, P], "mps", tag="wide")
         nc.tensor.transpose(mps[:], mpad[:], ident[:])
         mcol = keep.tile([P, NT], F32, name="mcol")
         nc.vector.tensor_copy(out=mcol[:], in_=mps[:, 0:NT])
@@ -105,7 +105,7 @@ def tile_graphlearner_pa_kernel(tc, feat, mask, W, b, out):
             fgs.append(fg)
             fg32 = fg[:].bitcast(F32).rearrange("p (n u) -> p n u", u=2)
             for hh in range(2):
-                tp = bank([P, 2, 256], "tp", tag="turn" if hh else "wide")
+                tp = bank([P, 2, 256], "tp", tag="wide")
                 for tt in range(2):
                     t = 4 * k + 2 * hh + tt
                     f32v = fraw[:, t, :].bitcast(F32)
@@ -164,7 +164,6 @@ def tile_graphlearner_pa_kernel(tc, feat, mask, W, b, out):
         nc.scalar.add(out=degs[:, :, 4], in_=mcol[:], add=1e-8)
         deg = keep.tile([P, NT], F32, name="deg")
         sdeg = keep.tile([P, NT], F32, name="sdeg")
-        five = keep.tile([P, 5], F32, name="five")
         dcol = keep.tile([P, NT], F32, name="dcol")
         dbc = keep.tile([P, N], F32, name="dbc")
         rowengine = {(3, 3): "S"}
@@ -240,8 +239,9 @@ def tile_graphlearner_pa_kernel(tc, feat, mask, W, b, out):
             nc.vector.quantize_mx(out=wq[:].bitcast(FP8X4), scales=wqs[:], in_=wg[:].rearrange("p w j -> p (w j)"))
 
         def degrees(g):
-            for i in range(4 * g, 4 * g + 4):
-                nc.scalar.activation(out=five[:], in_=degs[:, i, :], func=ACT.Copy, accum_out=deg[:, i:i + 1])
+            nc.vector.tensor_reduce(
+                out=deg[:, 4 * g:4 * g + 4], in_=degs[:, 4 * g:4 * g + 4, :], axis=AX.X, op=ALU.add
+            )
             nc.scalar.sqrt(out=sdeg[:, 4 * g:4 * g + 4], in_=deg[:, 4 * g:4 * g + 4])
 
         def d_of(g):
@@ -251,7 +251,7 @@ def tile_graphlearner_pa_kernel(tc, feat, mask, W, b, out):
         dps = {}
 
         def spread_d(g):
-            dp = bank([P, D], "dp", tag="turn")
+            dp = bank([P, D], "dp", tag="wide")
             dps[g] = dp
             for j in range(4):
                 nc.tensor.transpose(
@@ -288,7 +288,7 @@ def tile_graphlearner_pa_kernel(tc, feat, mask, W, b, out):
             )
 
         def scale(c, nb):
-            z = work.tile([P, D, 4], BF16, name="z", tag="z", bufs=4, align_bytes=64)
+            z = work.tile([P, D, 4], BF16, name="z", tag="z", bufs=5, align_bytes=64)
             zs[(c, nb)] = z
             nc.vector.tensor_tensor(
                 out=z[:].rearrange("p (c i) j -> p c j i", i=4),
@@ -300,10 +300,10 @@ def tile_graphlearner_pa_kernel(tc, feat, mask, W, b, out):
         def mirror(c, nb, halves=range(2)):
             z = zs[(c, nb)]
             if (nb, c) not in zs:
-                zs[(nb, c)] = work.tile([P, D, 4], BF16, name="zm", tag="zm", bufs=3, align_bytes=64)
+                zs[(nb, c)] = work.tile([P, D, 4], BF16, name="zm", tag="zm", bufs=4, align_bytes=64)
             zm = zs[(nb, c)]
             for h in halves:
-                tb = bank([P, 4, 256], "tb", BF16, tag="turn")
+                tb = bank([P, 4, 256], "tb", BF16, tag="wide")
                 for j in range(4):
                     for jj in (2 * h, 2 * h + 1):
                         nc.tensor.transpose(
@@ -324,7 +324,7 @@ def tile_graphlearner_pa_kernel(tc, feat, mask, W, b, out):
         braws = [big.tile([P, 4, D], BF16, name="braw%d" % k, offset=EBASE + 29696 + 4096 * k) for k in range(4)]
 
         def bias(k, u):
-            bp = bank([P, D], "bp", tag="turn")
+            bp = bank([P, D], "bp", tag="wide")
             for tt in range(4):
                 nc.tensor.transpose(
                     bp[:, P * tt:P * tt + P], braws[k][:, tt, :].bitcast(F32)[:, P * u:P * u + P], diag[:, 4 * k + tt, :]
@@ -367,17 +367,17 @@ def tile_graphlearner_pa_kernel(tc, feat, mask, W, b, out):
 
         gram_of(0)
         turn_feat(0)
-        gram_of(1)
         turn_feat(1)
+        gram_of(1)
         gram_of(2)
         gram_of(3)
-        turn_feat(2)
         quantise_feat(0)
         weights()
         quantise_feat(1)
-        quantise_weights()
         norm_sums()
+        quantise_weights()
         nc.vector.reciprocal(out=rn[:], in_=nrm[:])
+        turn_feat(2)
         turn_feat(3)
         pre_sup(0, nc.scalar.copy)
         for k in range(2):
@@ -399,13 +399,16 @@ def tile_graphlearner_pa_kernel(tc, feat, mask, W, b, out):
         quantise_xn(7)
         edge_unit(0, 3, range(4), (1, 3))
         quantise_feat(2)
-        degrees(0)
         edge_unit(1, 1, range(4), (1, 3))
+        degrees(0)
         self_loops(0)
         edge_unit(1, 2)
         d_of(0)
-        quantise_feat(3)
         edge_unit(1, 3)
+        scale_rows(0, 2)
+        scale_rows(0, 3)
+        quantise_feat(3)
+        edge_unit(2, 3)
         self_loops(1)
         degrees(1)
         spread_d(0)
@@ -417,22 +420,19 @@ def tile_graphlearner_pa_kernel(tc, feat, mask, W, b, out):
         d_of(1)
         scale(0, 0)
         edge_unit(2, 0)
-        scale_rows(1, 1)
         spread_d(1)
         edge_unit(2, 1)
-        scale_rows(0, 2)
+        scale_rows(1, 2)
         keep_d(1)
+        scale_rows(1, 1)
         scale(0, 1)
         quantise(0, 0)
         pre_sup(1, nc.scalar.copy, [2, 3])
-        edge_unit(2, 3)
         degrees(2)
         scale(1, 1)
         quantise(0, 1)
         mirror(0, 1)
         edge_unit(3, 3)
-        scale_rows(0, 3)
-        scale_rows(1, 2)
         self_loops(2)
         d_of(2)
         quantise(1, 1)
@@ -460,38 +460,38 @@ def tile_graphlearner_pa_kernel(tc, feat, mask, W, b, out):
         spread_d(3)
         quantise(2, 1)
         keep_d(3)
-        pre_sup(3, nc.scalar.copy)
         scale_rows(2, 3)
         bias(2, 0)
         bias(2, 1)
+        bias(3, 0)
+        bias(3, 1)
         quantise_pre_sup(2)
         scale(0, 3)
         scale(1, 3)
-        quantise_pre_sup(3)
         passes(0, range(3))
+        pre_sup(3, nc.scalar.copy)
         mirror(0, 3)
         mirror(1, 3)
         bias(0, 0)
         scale(2, 3)
+        mirror(2, 3)
+        quantise_pre_sup(3)
         quantise(3, 0)
         scale(2, 2)
         bias(0, 1)
-        bias(1, 0)
-        bias(1, 1)
         scale_rows(3, 3)
         quantise(3, 1)
         passes(0, [3])
-        mirror(2, 3)
+        bias(1, 0)
+        bias(1, 1)
         passes(1, range(4), range(2))
         quantise(2, 2)
         finish(0)
         passes(1, range(4), range(2, 4))
-        scale(3, 3)
-        bias(3, 0)
-        bias(3, 1)
         quantise(3, 2)
-        finish(1)
         quantise(0, 3)
+        scale(3, 3)
+        finish(1)
         quantise(1, 3)
         passes(2, range(4))
         quantise(2, 3)

@@ -166,7 +166,7 @@ def tile_graphlearner_pa_kernel(tc, feat, mask, W, b, out):
         sdeg = keep.tile([P, NT], F32, name="sdeg")
         dcol = keep.tile([P, NT], F32, name="dcol")
         dbc = keep.tile([P, N], F32, name="dbc")
-        rowengine = {(3, 3): "S"}
+        rowengine = {(3, 3): "S", (2, 3): "S"}
         A = {}
         aq = {}
         aqs = {}
@@ -200,9 +200,11 @@ def tile_graphlearner_pa_kernel(tc, feat, mask, W, b, out):
                     nc.scalar.activation(out=row, in_=ep[:], func=ACT.Relu, accum_out=degs[:, i, nb:nb + 1])
 
         def self_loops(c):
-                for j in range(4):
-                    blk = A[(c, c)][:, j, P * j:P * j + P]
-                    nc.vector.tensor_tensor(out=blk, in0=blk, in1=diag[:, 4 * c + j, :], op=ALU.add)
+            flat = A[(c, c)][:].rearrange("p j n -> p (j n)")
+            three = flat[:, 0:3 * (D + P)].rearrange("p (j n) -> p j n", j=3)[:, :, 0:P]
+            last = A[(c, c)][:, 3, 3 * P:4 * P]
+            nc.vector.tensor_tensor(out=three, in0=three, in1=diag[:, 4 * c:4 * c + 3, :], op=ALU.add)
+            nc.vector.tensor_tensor(out=last, in0=last, in1=diag[:, 4 * c + 3, :], op=ALU.add)
 
 
         xgs = {}
@@ -371,8 +373,8 @@ def tile_graphlearner_pa_kernel(tc, feat, mask, W, b, out):
         gram_of(1)
         gram_of(2)
         gram_of(3)
-        quantise_feat(0)
         weights()
+        quantise_feat(0)
         quantise_feat(1)
         norm_sums()
         quantise_weights()
@@ -380,12 +382,15 @@ def tile_graphlearner_pa_kernel(tc, feat, mask, W, b, out):
         turn_feat(2)
         turn_feat(3)
         pre_sup(0, nc.scalar.copy)
-        for k in range(2):
-            scale_xn(2 * k)
-            scale_xn(2 * k + 1)
-            quantise_xn(2 * k)
-            quantise_xn(2 * k + 1)
+        scale_xn(0)
+        scale_xn(1)
+        quantise_xn(0)
+        quantise_xn(1)
         edge_unit(0, 0)
+        scale_xn(2)
+        quantise_xn(2)
+        scale_xn(3)
+        quantise_xn(3)
         edge_unit(1, 0)
         edge_unit(0, 1)
         scale_xn(4)
@@ -397,25 +402,26 @@ def tile_graphlearner_pa_kernel(tc, feat, mask, W, b, out):
         scale_xn(7)
         quantise_xn(6)
         quantise_xn(7)
+        quantise_pre_sup(0)
+        quantise_feat(3)
         edge_unit(0, 3, range(4), (1, 3))
         quantise_feat(2)
-        edge_unit(1, 1, range(4), (1, 3))
+        edge_unit(1, 1)
         degrees(0)
         self_loops(0)
+        self_loops(1)
         edge_unit(1, 2)
         d_of(0)
         edge_unit(1, 3)
+        pre_sup(1, nc.scalar.copy, [0, 1])
         scale_rows(0, 2)
         scale_rows(0, 3)
-        quantise_feat(3)
-        edge_unit(2, 3)
-        self_loops(1)
-        degrees(1)
         spread_d(0)
-        scale_rows(0, 0)
-        pre_sup(1, nc.scalar.copy, [0, 1])
-        edge_unit(2, 2)
         keep_d(0)
+        scale_rows(0, 0)
+        degrees(1)
+        edge_unit(2, 3)
+        edge_unit(2, 2)
         scale_rows(0, 1)
         d_of(1)
         scale(0, 0)
@@ -426,7 +432,6 @@ def tile_graphlearner_pa_kernel(tc, feat, mask, W, b, out):
         keep_d(1)
         scale_rows(1, 1)
         scale(0, 1)
-        quantise(0, 0)
         pre_sup(1, nc.scalar.copy, [2, 3])
         degrees(2)
         scale(1, 1)
@@ -438,7 +443,6 @@ def tile_graphlearner_pa_kernel(tc, feat, mask, W, b, out):
         quantise(1, 1)
         edge_unit(3, 0)
         scale_rows(2, 2)
-        quantise_pre_sup(0)
         spread_d(2)
         edge_unit(3, 1)
         quantise(1, 0)
@@ -451,6 +455,7 @@ def tile_graphlearner_pa_kernel(tc, feat, mask, W, b, out):
         mirror(0, 2)
         quantise(0, 2)
         degrees(3)
+        quantise(0, 0)
         mirror(1, 2)
         self_loops(3)
         d_of(3)

@@ -165,7 +165,6 @@ def tile_graphlearner_pa_kernel(tc, feat, mask, W, b, out):
         deg = keep.tile([P, NT], F32, name="deg")
         sdeg = keep.tile([P, NT], F32, name="sdeg")
         dcol = keep.tile([P, NT], F32, name="dcol")
-        dbc = keep.tile([P, N], F32, name="dbc")
         rowengine = {(3, 3): "S", (2, 3): "S"}
         A = {}
         aq = {}
@@ -235,7 +234,7 @@ def tile_graphlearner_pa_kernel(tc, feat, mask, W, b, out):
             for u in range(2):
                 for e in range(2):
                     eb = 2 * u + e
-                    nc.vector.tensor_copy(out=wg[:, P * eb:P * eb + P, :], in_=wv[:, u, e])
+                    nc.scalar.copy(out=wg[:, P * eb:P * eb + P, :], in_=wv[:, u, e])
 
         def quantise_weights():
             nc.vector.quantize_mx(out=wq[:].bitcast(FP8X4), scales=wqs[:], in_=wg[:].rearrange("p w j -> p (w j)"))
@@ -259,9 +258,6 @@ def tile_graphlearner_pa_kernel(tc, feat, mask, W, b, out):
                 nc.tensor.transpose(
                     dp[:, P * j:P * j + P], dcol[:, 4 * g + j:4 * g + j + 1].to_broadcast([P, P]), ident[:]
                 )
-
-        def keep_d(g):
-            nc.vector.tensor_copy(out=dbc[:, D * g:D * g + D], in_=dps[g][:])
 
         def scale_rows(c, nb):
             for j in range(4):
@@ -295,7 +291,7 @@ def tile_graphlearner_pa_kernel(tc, feat, mask, W, b, out):
             nc.vector.tensor_tensor(
                 out=z[:].rearrange("p (c i) j -> p c j i", i=4),
                 in0=A[(c, nb)][:].rearrange("p j (c i) -> p c j i", i=4),
-                in1=dbc[:, D * nb:D * nb + D].rearrange("p (c i) -> p c i", i=4).unsqueeze(2).to_broadcast([P, P, 4, 4]),
+                in1=dps[nb][:].rearrange("p (c i) -> p c i", i=4).unsqueeze(2).to_broadcast([P, P, 4, 4]),
                 op=ALU.mult,
             )
 
@@ -340,8 +336,8 @@ def tile_graphlearner_pa_kernel(tc, feat, mask, W, b, out):
         done = {}
 
         def passes(nb, cs, ets=range(4), tag="wide"):
-            for c in cs:
-                for et in ets:
+            for et in ets:
+                for c in cs:
                     first = (nb, et) not in acc
                     if first:
                         acc[(nb, et)] = bank([P, D], "acc", tag=tag)
@@ -417,7 +413,6 @@ def tile_graphlearner_pa_kernel(tc, feat, mask, W, b, out):
         scale_rows(0, 2)
         scale_rows(0, 3)
         spread_d(0)
-        keep_d(0)
         scale_rows(0, 0)
         degrees(1)
         edge_unit(2, 3)
@@ -429,32 +424,28 @@ def tile_graphlearner_pa_kernel(tc, feat, mask, W, b, out):
         spread_d(1)
         edge_unit(2, 1)
         scale_rows(1, 2)
-        keep_d(1)
         scale_rows(1, 1)
         scale(0, 1)
         pre_sup(1, nc.scalar.copy, [2, 3])
-        degrees(2)
         scale(1, 1)
-        quantise(0, 1)
         mirror(0, 1)
+        degrees(2)
         edge_unit(3, 3)
         self_loops(2)
         d_of(2)
         quantise(1, 1)
         edge_unit(3, 0)
-        scale_rows(2, 2)
         spread_d(2)
         edge_unit(3, 1)
         quantise(1, 0)
-        keep_d(2)
         scale_rows(1, 3)
         scale(0, 2)
         edge_unit(3, 2)
         scale(1, 2)
-        quantise_pre_sup(1)
+        scale_rows(2, 2)
         mirror(0, 2)
-        quantise(0, 2)
         degrees(3)
+        quantise(0, 1)
         quantise(0, 0)
         mirror(1, 2)
         self_loops(3)
@@ -464,26 +455,27 @@ def tile_graphlearner_pa_kernel(tc, feat, mask, W, b, out):
         pre_sup(2, nc.scalar.copy)
         spread_d(3)
         quantise(2, 1)
-        keep_d(3)
         scale_rows(2, 3)
         bias(2, 0)
         bias(2, 1)
         bias(3, 0)
         bias(3, 1)
-        quantise_pre_sup(2)
         scale(0, 3)
         scale(1, 3)
-        passes(0, range(3))
         pre_sup(3, nc.scalar.copy)
         mirror(0, 3)
         mirror(1, 3)
         bias(0, 0)
         scale(2, 3)
+        quantise(0, 2)
+        quantise_pre_sup(1)
+        quantise_pre_sup(2)
         mirror(2, 3)
         quantise_pre_sup(3)
         quantise(3, 0)
         scale(2, 2)
         bias(0, 1)
+        passes(0, range(3))
         scale_rows(3, 3)
         quantise(3, 1)
         passes(0, [3])

@@ -165,7 +165,7 @@ def tile_graphlearner_pa_kernel(tc, feat, mask, W, b, out):
         deg = keep.tile([P, NT], F32, name="deg")
         sdeg = keep.tile([P, NT], F32, name="sdeg")
         dcol = keep.tile([P, NT], F32, name="dcol")
-        rowengine = {(3, 3): "S", (2, 3): "S"}
+        rowengine = {(3, 3): "S"}
         A = {}
         aq = {}
         aqs = {}
@@ -234,7 +234,7 @@ def tile_graphlearner_pa_kernel(tc, feat, mask, W, b, out):
             for u in range(2):
                 for e in range(2):
                     eb = 2 * u + e
-                    nc.scalar.copy(out=wg[:, P * eb:P * eb + P, :], in_=wv[:, u, e])
+                    nc.vector.tensor_copy(out=wg[:, P * eb:P * eb + P, :], in_=wv[:, u, e])
 
         def quantise_weights():
             nc.vector.quantize_mx(out=wq[:].bitcast(FP8X4), scales=wqs[:], in_=wg[:].rearrange("p w j -> p (w j)"))
@@ -384,8 +384,8 @@ def tile_graphlearner_pa_kernel(tc, feat, mask, W, b, out):
         quantise_xn(1)
         edge_unit(0, 0)
         scale_xn(2)
-        quantise_xn(2)
         scale_xn(3)
+        quantise_xn(2)
         quantise_xn(3)
         edge_unit(1, 0)
         edge_unit(0, 1)
@@ -398,11 +398,10 @@ def tile_graphlearner_pa_kernel(tc, feat, mask, W, b, out):
         scale_xn(7)
         quantise_xn(6)
         quantise_xn(7)
-        quantise_pre_sup(0)
         quantise_feat(3)
-        edge_unit(0, 3, range(4), (1, 3))
         quantise_feat(2)
-        edge_unit(1, 1)
+        edge_unit(0, 3, range(4), (1, 3))
+        edge_unit(1, 1, range(4), (1, 3))
         degrees(0)
         self_loops(0)
         self_loops(1)
@@ -410,7 +409,6 @@ def tile_graphlearner_pa_kernel(tc, feat, mask, W, b, out):
         d_of(0)
         edge_unit(1, 3)
         pre_sup(1, nc.scalar.copy, [0, 1])
-        scale_rows(0, 2)
         scale_rows(0, 3)
         spread_d(0)
         scale_rows(0, 0)
@@ -424,8 +422,10 @@ def tile_graphlearner_pa_kernel(tc, feat, mask, W, b, out):
         spread_d(1)
         edge_unit(2, 1)
         scale_rows(1, 2)
+        quantise_pre_sup(0)
         scale_rows(1, 1)
         scale(0, 1)
+        scale_rows(0, 2)
         pre_sup(1, nc.scalar.copy, [2, 3])
         scale(1, 1)
         mirror(0, 1)
@@ -442,21 +442,19 @@ def tile_graphlearner_pa_kernel(tc, feat, mask, W, b, out):
         scale(0, 2)
         edge_unit(3, 2)
         scale(1, 2)
+        quantise(1, 2)
         scale_rows(2, 2)
         mirror(0, 2)
         degrees(3)
         quantise(0, 1)
         quantise(0, 0)
-        mirror(1, 2)
+        bias(0, 1)
         self_loops(3)
         d_of(3)
-        quantise(1, 2)
         quantise(2, 0)
         pre_sup(2, nc.scalar.copy)
         spread_d(3)
-        quantise(2, 1)
         scale_rows(2, 3)
-        bias(2, 0)
         bias(2, 1)
         bias(3, 0)
         bias(3, 1)
@@ -466,33 +464,34 @@ def tile_graphlearner_pa_kernel(tc, feat, mask, W, b, out):
         mirror(0, 3)
         mirror(1, 3)
         bias(0, 0)
+        mirror(1, 2)
         scale(2, 3)
-        quantise(0, 2)
         quantise_pre_sup(1)
         quantise_pre_sup(2)
         mirror(2, 3)
         quantise_pre_sup(3)
         quantise(3, 0)
         scale(2, 2)
-        bias(0, 1)
+        quantise(0, 2)
+        quantise(2, 1)
         passes(0, range(3))
         scale_rows(3, 3)
         quantise(3, 1)
         passes(0, [3])
         bias(1, 0)
         bias(1, 1)
-        passes(1, range(4), range(2))
+        bias(2, 0)
         quantise(2, 2)
         finish(0)
-        passes(1, range(4), range(2, 4))
+        passes(1, range(4))
         quantise(3, 2)
         quantise(0, 3)
         scale(3, 3)
-        finish(1)
         quantise(1, 3)
         passes(2, range(4))
         quantise(2, 3)
         quantise(3, 3)
+        finish(1)
         finish(2)
         passes(3, range(4))
         finish(3)

from contextlib import ExitStack

import concourse.mybir as mybir
from concourse.masks import make_identity

F32 = mybir.dt.float32
BF16 = mybir.dt.bfloat16
U32 = mybir.dt.uint32
U8 = mybir.dt.uint8
FP8X4 = mybir.dt.float8_e4m3fn_x4
ALU = mybir.AluOpType
ACT = mybir.ActivationFunctionType
AX = mybir.AxisListType

P = 128
N = 2048
D = 512
NT = N // P
FLOPS = 2 * N * N * D * 2 + 2 * N * D * D
ABLK = 8192
UPPER = [(c, nb) for c in range(4) for nb in range(c, 4)]
EBASE = len(UPPER) * ABLK


def tile_graphlearner_pa_kernel(tc, feat, mask, W, b, out):
    nc = tc.nc
    feat_v = feat.flatten_outer_dims().rearrange("(t p) d -> p t d", p=P)
    b_v = b.rearrange("(t p) e -> p t e", p=P)
    mask_v = mask.rearrange("o (t p) -> (o t) p", p=P)
    out_v = out.flatten_outer_dims().rearrange("(u r e) n -> u e r n", u=2, e=2)

    with ExitStack() as ctx:
        ctx.enter_context(tc.manual_schedule())
        big = ctx.enter_context(tc.tile_pool(name="big", bufs=1))
        keep = ctx.enter_context(tc.tile_pool(name="keep", bufs=1))
        work = ctx.enter_context(tc.tile_pool(name="work", bufs=2))
        psum = ctx.enter_context(tc.psum_pool(name="psum", bufs=8))

        banks = {"wide": 8}

        def bank(shape, name, dtype=F32, tag="wide"):
            return psum.tile(shape, dtype, name=name, tag=tag, bufs=banks[tag])

        def a_offset(c, nb):
            return UPPER.index((c, nb)) * ABLK

        mraw = keep.tile([NT, P], BF16, name="mraw")
        nc.sync.dma_start(out=mraw[:], in_=mask_v)
        fraw = big.tile([P, NT, D], BF16, name="fraw", offset=7 * ABLK)
        for k in range(4):
            nc.sync.dma_start(out=fraw[:, 4 * k:4 * k + 4, :], in_=feat_v[:, 4 * k:4 * k + 4, :])
        wraw = big.tile([P, 4, D], BF16, name="wraw", offset=4 * ABLK + 4096)
        for u in range(2):
            nc.sync.dma_start(
                out=wraw[:, 2 * u:2 * u + 2, :],
                in_=W[256 * u:256 * u + 256, :].rearrange("(q e) c -> q e c", e=2),
            )

        ident = keep.tile([P, P], F32, name="ident")
        make_identity(nc, ident[:])
        identb = keep.tile([P, P], BF16, name="identb")
        make_identity(nc, identb[:])
        warm = keep.tile([P, 2], F32, name="warm")
        nc.vector.memset(warm[:], 1.0)
        nc.scalar.sqrt(out=warm[:, 1:2], in_=warm[:, 0:1])

        mpad = keep.tile([P, P], F32, name="mpad")
        nc.vector.memset(mpad[:], 0.0)
        nc.vector.tensor_copy(out=mpad[0:NT, :], in_=mraw[:])
        mps = bank([P, P], "mps", tag="wide")
        nc.tensor.transpose(mps[:], mpad[:], ident[:])
        mcol = keep.tile([P, NT], F32, name="mcol")
        nc.vector.tensor_copy(out=mcol[:], in_=mps[:, 0:NT])
        diag = keep.tile([P, NT, P], F32, name="diag")
        for k in range(4):
            nc.vector.tensor_tensor(
                out=diag[:, 4 * k:4 * k + 4, :],
                in0=ident[:].unsqueeze(1).to_broadcast([P, 4, P]),
                in1=mcol[:, 4 * k:4 * k + 4].unsqueeze(2).to_broadcast([P, 4, P]),
                op=ALU.mult,
            )

        xq = keep.tile([P, N], U32, name="xq", align_bytes=64)
        xqs = keep.tile([P, N], U8, name="xqs", align_bytes=64)
        pq = keep.tile([P, 4, D], U32, name="pq", align_bytes=64)
        pqs = keep.tile([P, 4, D], U8, name="pqs", align_bytes=64)
        fq = big.tile([P, N], U32, name="fq", offset=EBASE, align_bytes=64)
        fqs = big.tile([P, N], U8, name="fqs", offset=EBASE + 8192, align_bytes=64)
        wq = big.tile([P, D], U32, name="wq", offset=EBASE + 10240, align_bytes=64)
        wqs = big.tile([P, D], U8, name="wqs", offset=EBASE + 12288, align_bytes=64)

        gram = [bank([P, P], "gram%d" % k, tag="wide") for k in range(4)]
        fgs = []

        def gram_of(k):
            for t in range(4 * k, 4 * k + 4):
                fv = fraw[:, t, :].rearrange("p (u q e) -> p u q e", u=2, e=2)
                for u in range(2):
                    for e in range(2):
                        s = fv[:, u, :, e]
                        nc.tensor.matmul(gram[2 * u + e][:], lhsT=s, rhs=s, start=(t == 0), stop=(t == NT - 1))

        def turn_feat(k):
            fg = big.tile([P, 4 * D], BF16, name="fg", tag="fg", bufs=4, offset=5 * ABLK, align_bytes=64)
            fgs.append(fg)
            fg32 = fg[:].bitcast(F32).rearrange("p (n u) -> p n u", u=2)
            for hh in range(2):
                tp = bank([P, 2, 256], "tp", tag="wide")
                for tt in range(2):
                    t = 4 * k + 2 * hh + tt
                    f32v = fraw[:, t, :].bitcast(F32)
                    for u in range(2):
                        nc.tensor.transpose(tp[:, u, P * tt:P * tt + P], f32v[:, P * u:P * u + P], diag[:, t, :])
                nc.scalar.copy(out=fg32[:, 256 * hh:256 * hh + 256, :], in_=tp[:].rearrange("p u n -> p n u"))

        junk = keep.tile([P, 4, P], F32, name="junk")
        n2 = keep.tile([P, 4], F32, name="n2")
        n2c = keep.tile([P, 4], F32, name="n2c")
        nrm = keep.tile([P, 4], F32, name="nrm")
        rn = keep.tile([P, 4], F32, name="rn")
        rn_b = rn[:].rearrange("p (u e) -> p u e", u=2).unsqueeze(1).to_broadcast([P, 256, 2, 2])

        def norm_sums():
            for k in range(4):
                nc.vector.scalar_tensor_tensor(
                    out=junk[:, k, :], in0=gram[k][:], scalar=1.0, in1=ident[:], op0=ALU.mult, op1=ALU.mult,
                    accum_out=n2[:, k:k + 1],
                )
            nc.vector.tensor_scalar_max(out=n2c[:], in0=n2[:], scalar1=1e-24)
            nc.scalar.sqrt(out=nrm[:], in_=n2c[:])

        def quantise_feat(k):
            nc.vector.quantize_mx(
                out=fq[:, D * k:D * k + D].bitcast(FP8X4), scales=fqs[:, D * k:D * k + D], in_=fgs[k][:]
            )

        pgs = {}

        def pre_sup(c, engine, ebs=range(4)):
            if c not in pgs:
                pgs[c] = big.tile([P, D, 4], BF16, name="pg", tag="pg", bufs=4, offset=EBASE + 13312, align_bytes=64)
            pg = pgs[c]
            for eb in ebs:
                pp = bank([P, 4, P], "pp")
                for j in range(4):
                    i = 4 * c + j
                    nc.tensor.matmul_mx(
                        out=pp[:, j, :],
                        lhsT=fq[:, P * i:P * i + P].bitcast(FP8X4),
                        lhsT_scale=fqs[:, P * i:P * i + P],
                        rhs=wq[:, P * eb:P * eb + P].bitcast(FP8X4),
                        rhs_scale=wqs[:, P * eb:P * eb + P],
                        start=True,
                        stop=True,
                    )
                engine(out=pg[:, P * eb:P * eb + P, :], in_=pp[:].rearrange("p j w -> p w j"))

        def quantise_pre_sup(c):
            nc.vector.quantize_mx(
                out=pq[:, c, :].bitcast(FP8X4), scales=pqs[:, c, :], in_=pgs[c][:].rearrange("p w j -> p (w j)")
            )

        degs = keep.tile([P, NT, 5], F32, name="degs")
        nc.scalar.add(out=degs[:, :, 4], in_=mcol[:], add=1e-8)
        deg = keep.tile([P, NT], F32, name="deg")
        sdeg = keep.tile([P, NT], F32, name="sdeg")
        dcol = keep.tile([P, NT], F32, name="dcol")
        rowengine = {(3, 3): "S"}
        A = {}
        aq = {}
        aqs = {}

        def edge_unit(c, nb, js=range(4), vec=()):
            if nb >= c and (c, nb) not in A:
                A[(c, nb)] = big.tile([P, 4, D], F32, name="A%d_%d" % (c, nb), offset=a_offset(c, nb))
            for j in js:
                i = 4 * c + j
                ep = bank([P, D], "ep")
                nc.tensor.matmul_mx(
                    out=ep[:],
                    lhsT=xq[:, P * i:P * i + P].bitcast(FP8X4),
                    lhsT_scale=xqs[:, P * i:P * i + P],
                    rhs=xq[:, D * nb:D * nb + D].bitcast(FP8X4),
                    rhs_scale=xqs[:, D * nb:D * nb + D],
                    start=True,
                    stop=True,
                )
                if nb >= c:
                    row = A[(c, nb)][:, j, :]
                else:
                    unused = work.tile([P, D], BF16, name="unused", tag="unused", bufs=4)
                    row = unused[:]
                if j in vec:
                    nc.vector.tensor_scalar(
                        out=row, in0=ep[:], scalar1=0.0, scalar2=None, op0=ALU.max, op1=ALU.add,
                        accum_out=degs[:, i, nb:nb + 1],
                    )
                else:
                    nc.scalar.activation(out=row, in_=ep[:], func=ACT.Relu, accum_out=degs[:, i, nb:nb + 1])

        def self_loops(c):
            flat = A[(c, c)][:].rearrange("p j n -> p (j n)")
            three = flat[:, 0:3 * (D + P)].rearrange("p (j n) -> p j n", j=3)[:, :, 0:P]
            last = A[(c, c)][:, 3, 3 * P:4 * P]
            nc.vector.tensor_tensor(out=three, in0=three, in1=diag[:, 4 * c:4 * c + 3, :], op=ALU.add)
            nc.vector.tensor_tensor(out=last, in0=last, in1=diag[:, 4 * c + 3, :], op=ALU.add)


        xgs = {}

        def scale_xn(h):
            k, hh = divmod(h, 2)
            if hh == 0:
                xgs[k] = big.tile([P, 4 * D], BF16, name="xg", tag="xg", bufs=2, offset=9 * ABLK, align_bytes=64)
            half = slice(1024 * hh, 1024 * hh + 1024)
            nc.vector.tensor_tensor(
                out=xgs[k][:, half].rearrange("p (n u e) -> p n u e", u=2, e=2),
                in0=fgs[k][:, half].rearrange("p (n u e) -> p n u e", u=2, e=2),
                in1=rn_b,
                op=ALU.mult,
            )

        def quantise_xn(h):
            k, hh = divmod(h, 2)
            cols = slice(256 * h, 256 * h + 256)
            nc.vector.quantize_mx(
                out=xq[:, cols].bitcast(FP8X4), scales=xqs[:, cols], in_=xgs[k][:, 1024 * hh:1024 * hh + 1024]
            )

        wg = big.tile([P, D, 4], BF16, name="wg", offset=4 * ABLK, align_bytes=64)

        def weights():
            wv = wraw[:].rearrange("p j (u r e) -> p u e r j", u=2, e=2)
            for u in range(2):
                for e in range(2):
                    eb = 2 * u + e
                    nc.vector.tensor_copy(out=wg[:, P * eb:P * eb + P, :], in_=wv[:, u, e])

        def quantise_weights():
            nc.vector.quantize_mx(out=wq[:].bitcast(FP8X4), scales=wqs[:], in_=wg[:].rearrange("p w j -> p (w j)"))

        def degrees(g):
            nc.vector.tensor_reduce(
                out=deg[:, 4 * g:4 * g + 4], in_=degs[:, 4 * g:4 * g + 4, :], axis=AX.X, op=ALU.add
            )
            nc.scalar.sqrt(out=sdeg[:, 4 * g:4 * g + 4], in_=deg[:, 4 * g:4 * g + 4])

        def d_of(g):
            cols = slice(4 * g, 4 * g + 4)
            nc.vector.reciprocal(out=dcol[:, cols], in_=sdeg[:, cols])

        dps = {}

        def spread_d(g):
            dp = bank([P, D], "dp", tag="wide")
            dps[g] = dp
            for j in range(4):
                nc.tensor.transpose(
                    dp[:, P * j:P * j + P], dcol[:, 4 * g + j:4 * g + j + 1].to_broadcast([P, P]), ident[:]
                )

        def scale_rows(c, nb):
            for j in range(4):
                row = A[(c, nb)][:, j, :]
                d = dcol[:, 4 * c + j:4 * c + j + 1]
                who = rowengine.get((c, nb), "V")
                if who == "S":
                    nc.scalar.activation(out=row, in_=row, func=ACT.Copy, scale=d)
                else:
                    nc.vector.tensor_scalar_mul(out=row, in0=row, scalar1=d)

        zs = {}

        def quantise(c, nb):
            if nb >= c:
                off = a_offset(c, nb)
                aq[(c, nb)] = big.tile([P, D], U32, name="aq%d_%d" % (c, nb), offset=off, align_bytes=64)
                aqs[(c, nb)] = big.tile([P, D], U8, name="aqs%d_%d" % (c, nb), offset=off + 2048, align_bytes=64)
            else:
                aq[(c, nb)] = keep.tile([P, D], U32, name="aq%d_%d" % (c, nb), align_bytes=64)
                aqs[(c, nb)] = keep.tile([P, D], U8, name="aqs%d_%d" % (c, nb), align_bytes=64)
            nc.vector.quantize_mx(
                out=aq[(c, nb)][:].bitcast(FP8X4),
                scales=aqs[(c, nb)][:],
                in_=zs[(c, nb)][:].rearrange("p n j -> p (n j)"),
            )

        def scale(c, nb):
            z = work.tile([P, D, 4], BF16, name="z", tag="z", bufs=5, align_bytes=64)
            zs[(c, nb)] = z
            nc.vector.tensor_tensor(
                out=z[:].rearrange("p (c i) j -> p c j i", i=4),
                in0=A[(c, nb)][:].rearrange("p j (c i) -> p c j i", i=4),
                in1=dps[nb][:].rearrange("p (c i) -> p c i", i=4).unsqueeze(2).to_broadcast([P, P, 4, 4]),
                op=ALU.mult,
            )

        def mirror(c, nb, halves=range(2)):
            z = zs[(c, nb)]
            if (nb, c) not in zs:
                zs[(nb, c)] = work.tile([P, D, 4], BF16, name="zm", tag="zm", bufs=4, align_bytes=64)
            zm = zs[(nb, c)]
            for h in halves:
                tb = bank([P, 4, 256], "tb", BF16, tag="wide")
                for j in range(4):
                    for jj in (2 * h, 2 * h + 1):
                        nc.tensor.transpose(
                            tb[:, j, P * (jj - 2 * h):P * (jj - 2 * h) + P], z[:, P * j:P * j + P, jj], identb[:]
                        )
                nc.scalar.copy(out=zm[:, 256 * h:256 * h + 256, :], in_=tb[:].rearrange("p j n -> p n j"))

        def block(c, nb):
            scale(c, nb)
            if c < nb:
                mirror(c, nb)
            quantise(c, nb)
            if c < nb:
                quantise(nb, c)

        bT = keep.tile([P, 2, 2 * N], BF16, name="bT")

        braws = [big.tile([P, 4, D], BF16, name="braw%d" % k, offset=EBASE + 29696 + 4096 * k) for k in range(4)]

        def bias(k, u):
            bp = bank([P, D], "bp", tag="wide")
            for tt in range(4):
                nc.tensor.transpose(
                    bp[:, P * tt:P * tt + P], braws[k][:, tt, :].bitcast(F32)[:, P * u:P * u + P], diag[:, 4 * k + tt, :]
                )
            nc.scalar.copy(out=bT[:, u, 2 * D * k:2 * D * k + 2 * D], in_=bp[:].bitcast(BF16))

        for k in range(4):
            nc.sync.dma_start(out=braws[k][:], in_=b_v[:, 4 * k:4 * k + 4, :])

        acc = {}
        done = {}

        def passes(nb, cs, ets=range(4), tag="wide"):
            for et in ets:
                for c in cs:
                    first = (nb, et) not in acc
                    if first:
                        acc[(nb, et)] = bank([P, D], "acc", tag=tag)
                        done[(nb, et)] = 0
                    done[(nb, et)] += 1
                    nc.tensor.matmul_mx(
                        out=acc[(nb, et)][:],
                        lhsT=pq[:, c, P * et:P * et + P].bitcast(FP8X4),
                        lhsT_scale=pqs[:, c, P * et:P * et + P],
                        rhs=aq[(c, nb)][:].bitcast(FP8X4),
                        rhs_scale=aqs[(c, nb)][:],
                        start=first,
                        stop=(done[(nb, et)] == 4),
                    )

        def finish(nb):
            for u in range(2):
                for e in range(2):
                    y = big.tile([P, D], F32, name="y", tag="y", bufs=8, offset=EBASE + 29696)
                    bview = bT[:, u, 2 * D * nb:2 * D * nb + 2 * D].rearrange("p (n e) -> p n e", e=2)
                    nc.vector.tensor_tensor(out=y[:], in0=acc[(nb, 2 * u + e)][:], in1=bview[:, :, e], op=ALU.add)
                    nc.scalar.activation(out=y[:], in_=y[:], func=ACT.Tanh)
                    nc.sync.dma_start(out=out_v[u, e][:, D * nb:D * nb + D], in_=y[:])


        gram_of(0)
        turn_feat(0)
        turn_feat(1)
        gram_of(1)
        gram_of(2)
        gram_of(3)
        weights()
        quantise_feat(0)
        quantise_feat(1)
        norm_sums()
        quantise_weights()
        nc.vector.reciprocal(out=rn[:], in_=nrm[:])
        turn_feat(2)
        turn_feat(3)
        pre_sup(0, nc.scalar.copy)
        scale_xn(0)
        scale_xn(1)
        quantise_xn(0)
        quantise_xn(1)
        edge_unit(0, 0)
        scale_xn(2)
        scale_xn(3)
        quantise_xn(2)
        quantise_xn(3)
        edge_unit(1, 0)
        edge_unit(0, 1)
        scale_xn(4)
        scale_xn(5)
        quantise_xn(4)
        quantise_xn(5)
        edge_unit(0, 2)
        scale_xn(6)
        scale_xn(7)
        quantise_xn(6)
        quantise_xn(7)
        quantise_feat(3)
        quantise_feat(2)
        edge_unit(0, 3, range(4), (1, 3))
        edge_unit(1, 1, range(4), (1, 3))
        degrees(0)
        self_loops(0)
        self_loops(1)
        edge_unit(1, 2)
        d_of(0)
        edge_unit(1, 3)
        pre_sup(1, nc.scalar.copy, [0, 1])
        scale_rows(0, 3)
        spread_d(0)
        scale_rows(0, 0)
        degrees(1)
        edge_unit(2, 3)
        edge_unit(2, 2)
        scale_rows(0, 1)
        d_of(1)
        scale(0, 0)
        edge_unit(2, 0)
        spread_d(1)
        edge_unit(2, 1)
        scale_rows(1, 2)
        quantise_pre_sup(0)
        scale_rows(1, 1)
        scale(0, 1)
        scale_rows(0, 2)
        pre_sup(1, nc.scalar.copy, [2, 3])
        scale(1, 1)
        mirror(0, 1)
        degrees(2)
        edge_unit(3, 3)
        self_loops(2)
        d_of(2)
        quantise(1, 1)
        edge_unit(3, 0)
        spread_d(2)
        edge_unit(3, 1)
        quantise(1, 0)
        scale_rows(1, 3)
        scale(0, 2)
        edge_unit(3, 2)
        scale(1, 2)
        quantise(1, 2)
        scale_rows(2, 2)
        mirror(0, 2)
        degrees(3)
        quantise(0, 1)
        quantise(0, 0)
        bias(0, 1)
        self_loops(3)
        d_of(3)
        quantise(2, 0)
        pre_sup(2, nc.scalar.copy)
        spread_d(3)
        scale_rows(2, 3)
        bias(2, 1)
        bias(3, 0)
        bias(3, 1)
        scale(0, 3)
        scale(1, 3)
        pre_sup(3, nc.scalar.copy)
        mirror(0, 3)
        mirror(1, 3)
        bias(0, 0)
        mirror(1, 2)
        scale(2, 3)
        quantise_pre_sup(1)
        quantise_pre_sup(2)
        mirror(2, 3)
        quantise_pre_sup(3)
        quantise(3, 0)
        scale(2, 2)
        quantise(0, 2)
        quantise(2, 1)
        passes(0, range(3))
        scale_rows(3, 3)
        quantise(3, 1)
        passes(0, [3])
        bias(1, 0)
        bias(1, 1)
        bias(2, 0)
        quantise(2, 2)
        finish(0)
        passes(1, range(4))
        quantise(3, 2)
        quantise(0, 3)
        scale(3, 3)
        quantise(1, 3)
        passes(2, range(4))
        quantise(2, 3)
        quantise(3, 3)
        finish(1)
        finish(2)
        passes(3, range(4))
        finish(3)
